import numpy as np
import ml_dtypes


def mxq(x, axis, fmt="e4m3"):
    dtype, down = {"e4m3": (ml_dtypes.float8_e4m3fn, 7), "e5m2": (ml_dtypes.float8_e5m2, 14)}[fmt]
    v = np.moveaxis(np.asarray(x, np.float32).astype(ml_dtypes.bfloat16).astype(np.float64), axis, -1)
    blocks = v.reshape(v.shape[:-1] + (-1, 32))
    amax = np.abs(blocks).max(-1, keepdims=True)
    byte = np.maximum(np.where(amax > 0, np.frexp(amax)[1] - 1 + 127, 0) - down, 1)
    scale = np.exp2(byte - 127.0)
    codes = (blocks / scale).astype(np.float32).astype(dtype).astype(np.float64)
    return np.moveaxis((codes * scale).reshape(v.shape), -1, axis)


WIDE = False


def mx_kscale(k):
    if not WIDE:
        return np.ones(k)
    levels = np.array([10, -10, 5, -5, 0])
    a = np.random.permutation(np.resize(levels, k // 512 * 4)).reshape(k // 512, 4)
    idx = np.arange(k)
    return np.exp2(a[idx // 512, idx % 128 // 32])


BF16 = ml_dtypes.bfloat16


def bf(x):
    return np.asarray(x, np.float32).astype(BF16)


def f64(x):
    return np.asarray(x).astype(np.float64)


E2M1 = np.array([0.0, 0.5, 1.0, 1.5, 2.0, 3.0, 4.0, 6.0, -0.0, -0.5, -1.0, -1.5, -2.0, -3.0, -4.0, -6.0])


def pack_weight(w, fmt):
    k, n = w.shape
    w = f64(bf(w)).reshape(k // 32, 32, n)
    amax = np.abs(w).max(1)
    if fmt == "e4m3":
        byte = np.frexp(amax)[1] - 1 + 127 - 7
    else:
        mant, ex = np.frexp(amax / 6.0)
        byte = np.where(mant > 0.5, ex, ex - 1) + 127
    byte = np.clip(np.where(amax > 0, byte, 1), 1, 254)
    scaled = (w * np.exp2(127.0 - byte)[:, None, :]).reshape(k, n).astype(np.float32)
    by_word = np.ascontiguousarray(scaled.reshape(k // 512, 128, 4, n).transpose(0, 1, 3, 2))
    if fmt == "e4m3":
        words = by_word.astype(ml_dtypes.float8_e4m3fn).view(np.uint8)
    else:
        c = by_word.astype(ml_dtypes.float4_e2m1fn).view(np.uint8) & 0xF
        words = c[..., 0::2] | (c[..., 1::2] << 4)
    return np.ascontiguousarray(words), np.ascontiguousarray(byte.astype(np.uint8).reshape(k // 512, 16, n))


def unpack_weight(words, scales, fmt):
    g, p, n, _ = words.shape
    if fmt == "e4m3":
        vals = np.ascontiguousarray(words).view(ml_dtypes.float8_e4m3fn).astype(np.float64)
    else:
        nib = np.empty((g, p, n, 4), np.uint8)
        nib[..., 0::2] = words & 0xF
        nib[..., 1::2] = words >> 4
        vals = E2M1[nib]
    vals = vals * np.repeat(np.exp2(scales.astype(np.float64) - 127.0), 8, axis=1)[..., None]
    return vals.transpose(0, 1, 3, 2).reshape(g * 512, n)

def pack4(w):
    words, scales = pack_weight(w, "e2m1")
    return words.reshape(words.shape[0], 128, -1), scales


def unpack4(words, scales):
    return unpack_weight(words.reshape(words.shape[0], 128, -1, 2), scales, "e2m1")


B, T, D, H, KVH, HD = 2, 64, 1024, 16, 4, 128
HALF = HD // 2
EPS = 1e-6
ROPE_BASE = 10000.0


def zc_rmsnorm(x, scale):
    rms = np.sqrt(np.mean(x ** 2, axis=-1, keepdims=True) + EPS)
    return (1.0 + scale) * x / rms


def apply_rope(x, cos, sin):
    t = x.shape[2]
    c = cos[:t][None, None, :, :]
    s = sin[:t][None, None, :, :]
    x1, x2 = x[..., :HALF], x[..., HALF:]
    return np.concatenate([x1 * c - x2 * s, x2 * c + x1 * s], axis=-1)


def setup_inputs():
    s = mx_kscale(D)
    inv_freq = 1.0 / (ROPE_BASE ** (np.arange(0, HALF) / HALF))
    ang = np.arange(T)[:, None] * inv_freq[None, :]
    q_input = bf(np.random.standard_normal((B, T, D)) * s)
    words, scales = pack4(np.random.standard_normal((D, H * HD)) / np.sqrt(D) / s[:, None])
    return {"q_input": q_input,
            "Wq_words": words, "Wq_scales": scales,
            "q_scale": bf(np.random.standard_normal(HD) * 0.2),
            "cos": bf(np.cos(ang)), "sin": bf(np.sin(ang))}


def reference(q_input, Wq_words, Wq_scales, q_scale, cos, sin):
    b = q_input.shape[0]
    q = mxq(f64(q_input), 2, "e4m3") @ unpack4(Wq_words, Wq_scales)
    q = q.reshape(b, -1, H, HD).transpose(0, 2, 1, 3)
    q = zc_rmsnorm(q, f64(q_scale))
    return apply_rope(q, f64(cos), f64(sin))

@@ -1,0 +1,139 @@
+from contextlib import ExitStack
+
+import concourse.mybir as mybir
+from concourse.masks import make_identity
+
+F32 = mybir.dt.float32
+BF16 = mybir.dt.bfloat16
+I32 = mybir.dt.int32
+U32 = mybir.dt.uint32
+U8 = mybir.dt.uint8
+FP8X4 = mybir.dt.float8_e4m3fn_x4
+FP4X4 = mybir.dt.float4_e2m1fn_x4
+ALU = mybir.AluOpType
+ACT = mybir.ActivationFunctionType
+
+B, T, D, H, HD = 2, 64, 1024, 16, 128
+HALF = HD // 2
+EPS = 1e-6
+P = 128
+K_PASS = 512
+PASSES = D // K_PASS
+N_OUT = H * HD
+N_BANK = 512
+HEADS_BANK = N_BANK // HD
+BANKS = N_OUT // N_BANK
+
+FLOPS = 2 * B * T * D * N_OUT
+
+
+def tile_multiheadattention_pa_s_kernel(tc, q_input, Wq_words, Wq_scales, q_scale, cos, sin, out):
+    nc = tc.nc
+    with ExitStack() as ctx:
+        keep = ctx.enter_context(tc.tile_pool(name="keep", bufs=1))
+        psum = ctx.enter_context(tc.psum_pool(name="psum", bufs=1))
+
+        x_sb = keep.tile([P, D], BF16)
+        nc.sync.dma_start(out=x_sb[:], in_=q_input.rearrange("b t k -> t b k"))
+
+        w_scales = keep.tile([P, PASSES, N_OUT], U8, align_bytes=64)
+        nc.vector.memset(w_scales[:].bitcast(I32), 0)
+        planes_i32 = w_scales[:].bitcast(I32)
+        scales_i32 = Wq_scales.bitcast(I32)
+        for r in range(4):
+            for low in range(2):
+                nc.sync.dma_start(
+                    out=planes_i32[32 * low + r : P : 64],
+                    in_=scales_i32[:, 4 * low + r : 16 : 8, :].rearrange("g q n -> q g n"),
+                )
+
+        w_words = keep.tile([P, PASSES, 2 * N_OUT], U8, align_bytes=64)
+        for c in range(BANKS):
+            cols = slice(2 * N_BANK * c, 2 * N_BANK * (c + 1))
+            nc.sync.dma_start(
+                out=w_words[:, :, cols].bitcast(I32),
+                in_=Wq_words[:, :, cols].bitcast(I32).rearrange("g p n -> p g n"),
+            )
+
+        trig = keep.tile([P, 2, HALF], BF16)
+        nc.scalar.dma_start(out=trig[:, 0, :], in_=cos.unsqueeze(1).to_broadcast([T, B, HALF]))
+        nc.scalar.dma_start(out=trig[:, 1, :], in_=sin.unsqueeze(1).to_broadcast([T, B, HALF]))
+        q_scale_sb = keep.tile([P, HD], BF16)
+        nc.scalar.dma_start(out=q_scale_sb[:], in_=q_scale.partition_broadcast(P))
+
+        one = keep.tile([P, 1], F32)
+        nc.vector.memset(one[:], 1.0)
+        unused = keep.tile([P, 1], F32)
+        nc.scalar.activation(out=unused[:], in_=one[:], func=ACT.Abs_reciprocal_sqrt)
+
+        gain = keep.tile([P, 2, HALF], F32)
+        nc.gpsimd.tensor_scalar(
+            out=gain[:].rearrange("p f j -> p (f j)"), in0=q_scale_sb[:], scalar1=1.0, scalar2=1.0, op0=ALU.mult, op1=ALU.add
+        )
+        tables = keep.tile([P, 2, 2, HALF], F32)
+        nc.gpsimd.tensor_tensor(
+            out=tables[:],
+            in0=trig[:].unsqueeze(2).to_broadcast([P, 2, 2, HALF]),
+            in1=gain[:].unsqueeze(1).to_broadcast([P, 2, 2, HALF]),
+            op=ALU.mult,
+        )
+
+        ident = keep.tile([P, P], F32)
+        make_identity(nc, ident[:])
+        x_words = x_sb[:].bitcast(F32)
+        xT = psum.tile([P, PASSES, 2, P], F32)
+        for g in range(PASSES):
+            for u in range(2):
+                nc.tensor.transpose(xT[:, g, u, :], x_words[:, 256 * g + u : 256 * (g + 1) : 2], ident[:])
+        grouped = keep.tile([P, PASSES * P * 4], BF16, align_bytes=64)
+        nc.vector.tensor_copy(
+            out=grouped[:].bitcast(F32).rearrange("p (g m u) -> p g m u", g=PASSES, u=2),
+            in_=xT[:].rearrange("p g u m -> p g m u"),
+        )
+        x_codes = keep.tile([P, PASSES * P], U32, align_bytes=64)
+        x_scales = keep.tile([P, PASSES * P], U8, align_bytes=64)
+        nc.vector.quantize_mx(out=x_codes[:].bitcast(FP8X4), scales=x_scales[:], in_=grouped[:])
+
+        squares = keep.tile([P, H, HD], F32)
+        sumsq = keep.tile([P, H], F32)
+        inv_rms = keep.tile([P, H], F32)
+        prods = keep.tile([P, H, 2, HD], F32)
+        o_sb = keep.tile([P, H, HD], F32)
+        for c in range(BANKS):
+            acc = psum.tile([P, HEADS_BANK, HD], F32, name="acc%d" % c)
+            for g in range(PASSES):
+                nc.tensor.matmul_mx(
+                    out=acc[:].rearrange("p h d -> p (h d)"),
+                    lhsT=x_codes[:, P * g : P * (g + 1)].bitcast(FP8X4),
+                    lhsT_scale=x_scales[:, P * g : P * (g + 1)],
+                    rhs=w_words[:, g, 2 * N_BANK * c : 2 * N_BANK * (c + 1)].bitcast(FP4X4),
+                    rhs_scale=w_scales[:, g, N_BANK * c : N_BANK * (c + 1)],
+                    start=(g == 0),
+                    stop=(g == PASSES - 1),
+                )
+            heads = slice(HEADS_BANK * c, HEADS_BANK * (c + 1))
+            for j in range(HEADS_BANK):
+                h = HEADS_BANK * c + j
+                nc.scalar.activation(out=squares[:, h, :], in_=acc[:, j, :], func=ACT.Square, accum_out=sumsq[:, h : h + 1])
+            nc.scalar.activation(
+                out=inv_rms[:, heads], in_=sumsq[:, heads], func=ACT.Abs_reciprocal_sqrt, scale=1.0 / HD, bias=EPS
+            )
+            for j in range(HEADS_BANK):
+                h = HEADS_BANK * c + j
+                nc.vector.scalar_tensor_tensor(
+                    out=prods[:, h, :, :],
+                    in0=acc[:, j, :].unsqueeze(1).to_broadcast([P, 2, HD]),
+                    scalar=inv_rms[:, h : h + 1],
+                    in1=tables[:].rearrange("p s f j -> p s (f j)"),
+                    op0=ALU.mult,
+                    op1=ALU.mult,
+                )
+            nc.gpsimd.tensor_tensor(
+                out=o_sb[:, heads, 0:HALF], in0=prods[:, heads, 0, 0:HALF], in1=prods[:, heads, 1, HALF:HD], op=ALU.subtract
+            )
+            nc.gpsimd.tensor_tensor(
+                out=o_sb[:, heads, HALF:HD], in0=prods[:, heads, 0, HALF:HD], in1=prods[:, heads, 1, 0:HALF], op=ALU.add
+            )
+            for j in range(HEADS_BANK):
+                h = HEADS_BANK * c + j
+                nc.sync.dma_start(out=out[:, h, :, :].rearrange("b t d -> t b d"), in_=o_sb[:, h, :])

@@ -20,9 +20,10 @@ P = 128
 K_PASS = 512
 PASSES = D // K_PASS
 N_OUT = H * HD
-N_BANK = 512
-HEADS_BANK = N_BANK // HD
-BANKS = N_OUT // N_BANK
+HEADS_BANK = 2
+HEADS_CHUNK = 4
+BANKS_CHUNK = HEADS_CHUNK // HEADS_BANK
+CHUNKS = H // HEADS_CHUNK
 
 FLOPS = 2 * B * T * D * N_OUT
 
@@ -31,109 +32,116 @@ def tile_multiheadattention_pa_s_kernel(tc, q_input, Wq_words, Wq_scales, q_scal
     nc = tc.nc
     with ExitStack() as ctx:
         keep = ctx.enter_context(tc.tile_pool(name="keep", bufs=1))
-        psum = ctx.enter_context(tc.psum_pool(name="psum", bufs=1))
+        psum = ctx.enter_context(tc.psum_pool(name="psum", bufs=8))
+        ctx.enter_context(tc.manual_schedule())
 
         x_sb = keep.tile([P, D], BF16)
-        nc.sync.dma_start(out=x_sb[:], in_=q_input.rearrange("b t k -> t b k"))
+        for g in range(PASSES):
+            k_cols = slice(K_PASS * g, K_PASS * (g + 1))
+            nc.sync.dma_start(out=x_sb[:, k_cols], in_=q_input[:, :, k_cols].rearrange("b t k -> t b k"))
 
         w_scales = keep.tile([P, PASSES, N_OUT], U8, align_bytes=64)
         nc.vector.memset(w_scales[:].bitcast(I32), 0)
         planes_i32 = w_scales[:].bitcast(I32)
         scales_i32 = Wq_scales.bitcast(I32)
         for r in range(4):
-            for low in range(2):
-                nc.sync.dma_start(
-                    out=planes_i32[32 * low + r : P : 64],
-                    in_=scales_i32[:, 4 * low + r : 16 : 8, :].rearrange("g q n -> q g n"),
-                )
+            nc.sync.dma_start(out=planes_i32[r:P:32], in_=scales_i32[:, r:16:4, :].rearrange("g q n -> q g n"))
 
         w_words = keep.tile([P, PASSES, 2 * N_OUT], U8, align_bytes=64)
-        for c in range(BANKS):
-            cols = slice(2 * N_BANK * c, 2 * N_BANK * (c + 1))
+        for c in range(CHUNKS):
+            w_bytes = slice(2 * HD * HEADS_CHUNK * c, 2 * HD * HEADS_CHUNK * (c + 1))
             nc.sync.dma_start(
-                out=w_words[:, :, cols].bitcast(I32),
-                in_=Wq_words[:, :, cols].bitcast(I32).rearrange("g p n -> p g n"),
+                out=w_words[:, :, w_bytes].bitcast(I32),
+                in_=Wq_words[:, :, w_bytes].bitcast(I32).rearrange("g p n -> p g n"),
             )
 
+        ident = keep.tile([P, P], F32)
+        make_identity(nc, ident[:])
         trig = keep.tile([P, 2, HALF], BF16)
-        nc.scalar.dma_start(out=trig[:, 0, :], in_=cos.unsqueeze(1).to_broadcast([T, B, HALF]))
-        nc.scalar.dma_start(out=trig[:, 1, :], in_=sin.unsqueeze(1).to_broadcast([T, B, HALF]))
+        nc.gpsimd.dma_start(out=trig[:, 0, :], in_=cos.unsqueeze(1).to_broadcast([T, B, HALF]))
+        nc.gpsimd.dma_start(out=trig[:, 1, :], in_=sin.unsqueeze(1).to_broadcast([T, B, HALF]))
         q_scale_sb = keep.tile([P, HD], BF16)
-        nc.scalar.dma_start(out=q_scale_sb[:], in_=q_scale.partition_broadcast(P))
+        nc.gpsimd.dma_start(out=q_scale_sb[:], in_=q_scale.partition_broadcast(P))
 
         one = keep.tile([P, 1], F32)
         nc.vector.memset(one[:], 1.0)
         unused = keep.tile([P, 1], F32)
         nc.scalar.activation(out=unused[:], in_=one[:], func=ACT.Abs_reciprocal_sqrt)
 
+        x_words = x_sb[:].bitcast(F32)
+        grouped = keep.tile([P, PASSES, 4 * P], BF16, align_bytes=64)
+        x_codes = keep.tile([P, PASSES, P], U32, align_bytes=64)
+        x_scales = keep.tile([P, PASSES, P], U8, align_bytes=64)
+        copy_out = [nc.vector.tensor_copy, nc.scalar.copy]
+        for g in range(PASSES):
+            xT = psum.tile([P, 2, P], F32, name="xT%d" % g, tag="bank")
+            for u in range(2):
+                nc.tensor.transpose(xT[:, u, :], x_words[:, 256 * g + u : 256 * (g + 1) : 2], ident[:])
+            copy_out[g](
+                out=grouped[:, g, :].bitcast(F32).rearrange("p (m u) -> p m u", u=2),
+                in_=xT[:].rearrange("p u m -> p m u"),
+            )
+            nc.vector.quantize_mx(out=x_codes[:, g, :].bitcast(FP8X4), scales=x_scales[:, g, :], in_=grouped[:, g, :])
+
         gain = keep.tile([P, 2, HALF], F32)
-        nc.gpsimd.tensor_scalar(
+        nc.vector.tensor_scalar(
             out=gain[:].rearrange("p f j -> p (f j)"), in0=q_scale_sb[:], scalar1=1.0, scalar2=1.0, op0=ALU.mult, op1=ALU.add
         )
         tables = keep.tile([P, 2, 2, HALF], F32)
-        nc.gpsimd.tensor_tensor(
+        nc.vector.tensor_tensor(
             out=tables[:],
             in0=trig[:].unsqueeze(2).to_broadcast([P, 2, 2, HALF]),
             in1=gain[:].unsqueeze(1).to_broadcast([P, 2, 2, HALF]),
             op=ALU.mult,
         )
 
-        ident = keep.tile([P, P], F32)
-        make_identity(nc, ident[:])
-        x_words = x_sb[:].bitcast(F32)
-        xT = psum.tile([P, PASSES, 2, P], F32)
-        for g in range(PASSES):
-            for u in range(2):
-                nc.tensor.transpose(xT[:, g, u, :], x_words[:, 256 * g + u : 256 * (g + 1) : 2], ident[:])
-        grouped = keep.tile([P, PASSES * P * 4], BF16, align_bytes=64)
-        nc.vector.tensor_copy(
-            out=grouped[:].bitcast(F32).rearrange("p (g m u) -> p g m u", g=PASSES, u=2),
-            in_=xT[:].rearrange("p g u m -> p g m u"),
-        )
-        x_codes = keep.tile([P, PASSES * P], U32, align_bytes=64)
-        x_scales = keep.tile([P, PASSES * P], U8, align_bytes=64)
-        nc.vector.quantize_mx(out=x_codes[:].bitcast(FP8X4), scales=x_scales[:], in_=grouped[:])
-
         squares = keep.tile([P, H, HD], F32)
         sumsq = keep.tile([P, H], F32)
         inv_rms = keep.tile([P, H], F32)
         prods = keep.tile([P, H, 2, HD], F32)
         o_sb = keep.tile([P, H, HD], F32)
-        for c in range(BANKS):
-            acc = psum.tile([P, HEADS_BANK, HD], F32, name="acc%d" % c)
-            for g in range(PASSES):
-                nc.tensor.matmul_mx(
-                    out=acc[:].rearrange("p h d -> p (h d)"),
-                    lhsT=x_codes[:, P * g : P * (g + 1)].bitcast(FP8X4),
-                    lhsT_scale=x_scales[:, P * g : P * (g + 1)],
-                    rhs=w_words[:, g, 2 * N_BANK * c : 2 * N_BANK * (c + 1)].bitcast(FP4X4),
-                    rhs_scale=w_scales[:, g, N_BANK * c : N_BANK * (c + 1)],
-                    start=(g == 0),
-                    stop=(g == PASSES - 1),
+        for c in range(CHUNKS):
+            for i in range(BANKS_CHUNK):
+                first = HEADS_CHUNK * c + HEADS_BANK * i
+                acc = psum.tile([P, HEADS_BANK, HD], F32, name="acc%d" % first, tag="bank")
+                for j in range(HEADS_BANK):
+                    h = first + j
+                    for g in range(PASSES):
+                        nc.tensor.matmul_mx(
+                            out=acc[:, j, :],
+                            lhsT=x_codes[:, g, :].bitcast(FP8X4),
+                            lhsT_scale=x_scales[:, g, :],
+                            rhs=w_words[:, g, 2 * HD * h : 2 * HD * (h + 1)].bitcast(FP4X4),
+                            rhs_scale=w_scales[:, g, HD * h : HD * (h + 1)],
+                            start=(g == 0),
+                            stop=(g == PASSES - 1),
+                        )
+                for j in range(HEADS_BANK):
+                    h = first + j
+                    nc.scalar.activation(
+                        out=squares[:, h, :], in_=acc[:, j, :], func=ACT.Square, accum_out=sumsq[:, h : h + 1]
+                    )
+                pair = slice(first, first + HEADS_BANK)
+                nc.scalar.activation(
+                    out=inv_rms[:, pair], in_=sumsq[:, pair], func=ACT.Abs_reciprocal_sqrt, scale=1.0 / HD, bias=EPS
                 )
-            heads = slice(HEADS_BANK * c, HEADS_BANK * (c + 1))
-            for j in range(HEADS_BANK):
-                h = HEADS_BANK * c + j
-                nc.scalar.activation(out=squares[:, h, :], in_=acc[:, j, :], func=ACT.Square, accum_out=sumsq[:, h : h + 1])
-            nc.scalar.activation(
-                out=inv_rms[:, heads], in_=sumsq[:, heads], func=ACT.Abs_reciprocal_sqrt, scale=1.0 / HD, bias=EPS
-            )
-            for j in range(HEADS_BANK):
-                h = HEADS_BANK * c + j
-                nc.vector.scalar_tensor_tensor(
-                    out=prods[:, h, :, :],
-                    in0=acc[:, j, :].unsqueeze(1).to_broadcast([P, 2, HD]),
-                    scalar=inv_rms[:, h : h + 1],
-                    in1=tables[:].rearrange("p s f j -> p s (f j)"),
-                    op0=ALU.mult,
-                    op1=ALU.mult,
-                )
-            nc.gpsimd.tensor_tensor(
+                for j in range(HEADS_BANK):
+                    h = first + j
+                    nc.vector.scalar_tensor_tensor(
+                        out=prods[:, h, :, :],
+                        in0=acc[:, j, :].unsqueeze(1).to_broadcast([P, 2, HD]),
+                        scalar=inv_rms[:, h : h + 1],
+                        in1=tables[:].rearrange("p s f j -> p s (f j)"),
+                        op0=ALU.mult,
+                        op1=ALU.mult,
+                    )
+            adder = nc.gpsimd if c < CHUNKS - 1 else nc.vector
+            heads = slice(HEADS_CHUNK * c, HEADS_CHUNK * (c + 1))
+            adder.tensor_tensor(
                 out=o_sb[:, heads, 0:HALF], in0=prods[:, heads, 0, 0:HALF], in1=prods[:, heads, 1, HALF:HD], op=ALU.subtract
             )
-            nc.gpsimd.tensor_tensor(
+            adder.tensor_tensor(
                 out=o_sb[:, heads, HALF:HD], in0=prods[:, heads, 0, HALF:HD], in1=prods[:, heads, 1, 0:HALF], op=ALU.add
             )
-            for j in range(HEADS_BANK):
-                h = HEADS_BANK * c + j
+            for h in range(HEADS_CHUNK * c, HEADS_CHUNK * (c + 1)):
                 nc.sync.dma_start(out=out[:, h, :, :].rearrange("b t d -> t b d"), in_=o_sb[:, h, :])

@@ -35,6 +35,12 @@ def tile_multiheadattention_pa_s_kernel(tc, q_input, Wq_words, Wq_scales, q_scal
         psum = ctx.enter_context(tc.psum_pool(name="psum", bufs=8))
         ctx.enter_context(tc.manual_schedule())
 
+        q_scale_sb = keep.tile([P, HD], BF16)
+        nc.scalar.dma_start(out=q_scale_sb[:], in_=q_scale.partition_broadcast(P))
+        trig = keep.tile([P, 2, HALF], BF16)
+        nc.scalar.dma_start(out=trig[:, 0, :], in_=cos.unsqueeze(1).to_broadcast([T, B, HALF]))
+        nc.scalar.dma_start(out=trig[:, 1, :], in_=sin.unsqueeze(1).to_broadcast([T, B, HALF]))
+
         x_sb = keep.tile([P, D], BF16)
         for g in range(PASSES):
             k_cols = slice(K_PASS * g, K_PASS * (g + 1))
@@ -57,11 +63,6 @@ def tile_multiheadattention_pa_s_kernel(tc, q_input, Wq_words, Wq_scales, q_scal
 
         ident = keep.tile([P, P], F32)
         make_identity(nc, ident[:])
-        trig = keep.tile([P, 2, HALF], BF16)
-        nc.gpsimd.dma_start(out=trig[:, 0, :], in_=cos.unsqueeze(1).to_broadcast([T, B, HALF]))
-        nc.gpsimd.dma_start(out=trig[:, 1, :], in_=sin.unsqueeze(1).to_broadcast([T, B, HALF]))
-        q_scale_sb = keep.tile([P, HD], BF16)
-        nc.gpsimd.dma_start(out=q_scale_sb[:], in_=q_scale.partition_broadcast(P))
 
         one = keep.tile([P, 1], F32)
         nc.vector.memset(one[:], 1.0)

@@ -35,12 +35,6 @@ def tile_multiheadattention_pa_s_kernel(tc, q_input, Wq_words, Wq_scales, q_scal
         psum = ctx.enter_context(tc.psum_pool(name="psum", bufs=8))
         ctx.enter_context(tc.manual_schedule())
 
-        q_scale_sb = keep.tile([P, HD], BF16)
-        nc.scalar.dma_start(out=q_scale_sb[:], in_=q_scale.partition_broadcast(P))
-        trig = keep.tile([P, 2, HALF], BF16)
-        nc.scalar.dma_start(out=trig[:, 0, :], in_=cos.unsqueeze(1).to_broadcast([T, B, HALF]))
-        nc.scalar.dma_start(out=trig[:, 1, :], in_=sin.unsqueeze(1).to_broadcast([T, B, HALF]))
-
         x_sb = keep.tile([P, D], BF16)
         for g in range(PASSES):
             k_cols = slice(K_PASS * g, K_PASS * (g + 1))
@@ -63,6 +57,14 @@ def tile_multiheadattention_pa_s_kernel(tc, q_input, Wq_words, Wq_scales, q_scal
 
         ident = keep.tile([P, P], F32)
         make_identity(nc, ident[:])
+        q_scale_row = keep.tile([P, HD], BF16)
+        nc.vector.memset(q_scale_row[:], 0.0)
+        nc.gpsimd.dma_start(out=q_scale_row[0:1, :], in_=q_scale.unsqueeze(0))
+        trig = keep.tile([P, 2, HALF], BF16)
+        nc.gpsimd.dma_start(out=trig[:, 0, :], in_=cos.unsqueeze(1).to_broadcast([T, B, HALF]))
+        nc.gpsimd.dma_start(out=trig[:, 1, :], in_=sin.unsqueeze(1).to_broadcast([T, B, HALF]))
+        ones = keep.tile([P, P], BF16)
+        nc.vector.memset(ones[:], 1.0)
 
         one = keep.tile([P, 1], F32)
         nc.vector.memset(one[:], 1.0)
@@ -84,9 +86,11 @@ def tile_multiheadattention_pa_s_kernel(tc, q_input, Wq_words, Wq_scales, q_scal
             )
             nc.vector.quantize_mx(out=x_codes[:, g, :].bitcast(FP8X4), scales=x_scales[:, g, :], in_=grouped[:, g, :])
 
+        q_scale_ps = psum.tile([P, HD], F32, tag="bank")
+        nc.tensor.matmul(out=q_scale_ps[:], lhsT=ones[:], rhs=q_scale_row[:], start=True, stop=True)
         gain = keep.tile([P, 2, HALF], F32)
         nc.vector.tensor_scalar(
-            out=gain[:].rearrange("p f j -> p (f j)"), in0=q_scale_sb[:], scalar1=1.0, scalar2=1.0, op0=ALU.mult, op1=ALU.add
+            out=gain[:].rearrange("p f j -> p (f j)"), in0=q_scale_ps[:], scalar1=1.0, scalar2=1.0, op0=ALU.mult, op1=ALU.add
         )
         tables = keep.tile([P, 2, 2, HALF], F32)
         nc.vector.tensor_tensor(

@@ -35,6 +35,9 @@ def tile_multiheadattention_pa_s_kernel(tc, q_input, Wq_words, Wq_scales, q_scal
         psum = ctx.enter_context(tc.psum_pool(name="psum", bufs=8))
         ctx.enter_context(tc.manual_schedule())
 
+        trig = keep.tile([P, 2, HALF], BF16)
+        nc.scalar.dma_start(out=trig[:, 1, :], in_=sin.unsqueeze(1).to_broadcast([T, B, HALF]))
+
         x_sb = keep.tile([P, D], BF16)
         for g in range(PASSES):
             k_cols = slice(K_PASS * g, K_PASS * (g + 1))
@@ -55,14 +58,12 @@ def tile_multiheadattention_pa_s_kernel(tc, q_input, Wq_words, Wq_scales, q_scal
                 in_=Wq_words[:, :, w_bytes].bitcast(I32).rearrange("g p n -> p g n"),
             )
 
+        q_scale_row = keep.tile([P, HD], BF16)
+        nc.gpsimd.memset(q_scale_row[:], 0.0)
+        nc.gpsimd.dma_start(out=q_scale_row[0:1, :], in_=q_scale.unsqueeze(0))
+        nc.gpsimd.dma_start(out=trig[:, 0, :], in_=cos.unsqueeze(1).to_broadcast([T, B, HALF]))
         ident = keep.tile([P, P], F32)
         make_identity(nc, ident[:])
-        q_scale_row = keep.tile([P, HD], BF16)
-        nc.vector.memset(q_scale_row[:], 0.0)
-        nc.gpsimd.dma_start(out=q_scale_row[0:1, :], in_=q_scale.unsqueeze(0))
-        trig = keep.tile([P, 2, HALF], BF16)
-        nc.gpsimd.dma_start(out=trig[:, 0, :], in_=cos.unsqueeze(1).to_broadcast([T, B, HALF]))
-        nc.gpsimd.dma_start(out=trig[:, 1, :], in_=sin.unsqueeze(1).to_broadcast([T, B, HALF]))
         ones = keep.tile([P, P], BF16)
         nc.vector.memset(ones[:], 1.0)
 

@@ -35,8 +35,9 @@ def tile_multiheadattention_pa_s_kernel(tc, q_input, Wq_words, Wq_scales, q_scal
         psum = ctx.enter_context(tc.psum_pool(name="psum", bufs=8))
         ctx.enter_context(tc.manual_schedule())
 
-        trig = keep.tile([P, 2, HALF], BF16)
-        nc.scalar.dma_start(out=trig[:, 1, :], in_=sin.unsqueeze(1).to_broadcast([T, B, HALF]))
+        q_scale_row = keep.tile([P, HD], BF16)
+        nc.vector.memset(q_scale_row[:], 0.0)
+        nc.scalar.dma_start(out=q_scale_row[0:1, :], in_=q_scale.unsqueeze(0))
 
         x_sb = keep.tile([P, D], BF16)
         for g in range(PASSES):
@@ -58,12 +59,11 @@ def tile_multiheadattention_pa_s_kernel(tc, q_input, Wq_words, Wq_scales, q_scal
                 in_=Wq_words[:, :, w_bytes].bitcast(I32).rearrange("g p n -> p g n"),
             )
 
-        q_scale_row = keep.tile([P, HD], BF16)
-        nc.gpsimd.memset(q_scale_row[:], 0.0)
-        nc.gpsimd.dma_start(out=q_scale_row[0:1, :], in_=q_scale.unsqueeze(0))
-        nc.gpsimd.dma_start(out=trig[:, 0, :], in_=cos.unsqueeze(1).to_broadcast([T, B, HALF]))
         ident = keep.tile([P, P], F32)
         make_identity(nc, ident[:])
+        trig = keep.tile([P, 2, HALF], BF16)
+        nc.gpsimd.dma_start(out=trig[:, 0, :], in_=cos.unsqueeze(1).to_broadcast([T, B, HALF]))
+        nc.gpsimd.dma_start(out=trig[:, 1, :], in_=sin.unsqueeze(1).to_broadcast([T, B, HALF]))
         ones = keep.tile([P, P], BF16)
         nc.vector.memset(ones[:], 1.0)
 
@@ -149,5 +149,5 @@ def tile_multiheadattention_pa_s_kernel(tc, q_input, Wq_words, Wq_scales, q_scal
             adder.tensor_tensor(
                 out=o_sb[:, heads, HALF:HD], in0=prods[:, heads, 0, HALF:HD], in1=prods[:, heads, 1, 0:HALF], op=ALU.add
             )
-            for h in range(HEADS_CHUNK * c, HEADS_CHUNK * (c + 1)):
-                nc.sync.dma_start(out=out[:, h, :, :].rearrange("b t d -> t b d"), in_=o_sb[:, h, :])
+            for b in range(B):
+                nc.sync.dma_start(out=out[b, heads, :, :].rearrange("h t d -> t h d"), in_=o_sb[b:P:B, heads, :])

@@ -20,10 +20,14 @@ P = 128
 K_PASS = 512
 PASSES = D // K_PASS
 N_OUT = H * HD
-HEADS_BANK = 2
 HEADS_CHUNK = 4
-BANKS_CHUNK = HEADS_CHUNK // HEADS_BANK
 CHUNKS = H // HEADS_CHUNK
+
+BANKS = [2,2,2,2,2,2,2,2]
+GROUPS = [[0,2,'g'],[2,5,'g'],[5,8,'g'],[8,11,'g'],[11,13,'g'],[13,16,'v']]
+ONE_ADD = True
+WARM = 0
+WARM_N = 128
 
 FLOPS = 2 * B * T * D * N_OUT
 
@@ -36,32 +40,38 @@ def tile_multiheadattention_pa_s_kernel(tc, q_input, Wq_words, Wq_scales, q_scal
         ctx.enter_context(tc.manual_schedule())
 
         q_scale_row = keep.tile([P, HD], BF16)
-        nc.vector.memset(q_scale_row[:], 0.0)
-        nc.scalar.dma_start(out=q_scale_row[0:1, :], in_=q_scale.unsqueeze(0))
-
         x_sb = keep.tile([P, D], BF16)
-        for g in range(PASSES):
-            k_cols = slice(K_PASS * g, K_PASS * (g + 1))
-            nc.sync.dma_start(out=x_sb[:, k_cols], in_=q_input[:, :, k_cols].rearrange("b t k -> t b k"))
-
         w_scales = keep.tile([P, PASSES, N_OUT], U8, align_bytes=64)
-        nc.vector.memset(w_scales[:].bitcast(I32), 0)
+        w_words = keep.tile([P, PASSES, 2 * N_OUT], U8, align_bytes=64)
+        trig = keep.tile([P, 2, HALF], BF16)
+        ident = keep.tile([P, P], F32)
         planes_i32 = w_scales[:].bitcast(I32)
         scales_i32 = Wq_scales.bitcast(I32)
-        for r in range(4):
-            nc.sync.dma_start(out=planes_i32[r:P:32], in_=scales_i32[:, r:16:4, :].rearrange("g q n -> q g n"))
 
-        w_words = keep.tile([P, PASSES, 2 * N_OUT], U8, align_bytes=64)
-        for c in range(CHUNKS):
-            w_bytes = slice(2 * HD * HEADS_CHUNK * c, 2 * HD * HEADS_CHUNK * (c + 1))
+        def load_x(queue, g):
+            k_cols = slice(K_PASS * g, K_PASS * (g + 1))
+            queue.dma_start(out=x_sb[:, k_cols], in_=q_input[:, :, k_cols].rearrange("b t k -> t b k"))
+
+        def load_scales():
+            for r in range(4):
+                nc.sync.dma_start(out=planes_i32[r:P:32], in_=scales_i32[:, r:16:4, :].rearrange("g q n -> q g n"))
+
+        def load_words(lo, hi):
+            w_bytes = slice(2 * HD * lo, 2 * HD * hi)
             nc.sync.dma_start(
                 out=w_words[:, :, w_bytes].bitcast(I32),
                 in_=Wq_words[:, :, w_bytes].bitcast(I32).rearrange("g p n -> p g n"),
             )
 
-        ident = keep.tile([P, P], F32)
+        nc.vector.memset(q_scale_row[:], 0.0)
+        nc.scalar.dma_start(out=q_scale_row[0:1, :], in_=q_scale.unsqueeze(0))
+        for g in range(PASSES):
+            load_x(nc.sync, g)
+        nc.vector.memset(w_scales[:].bitcast(I32), 0)
+        load_scales()
+        for c in range(CHUNKS):
+            load_words(HEADS_CHUNK * c, HEADS_CHUNK * (c + 1))
         make_identity(nc, ident[:])
-        trig = keep.tile([P, 2, HALF], BF16)
         nc.gpsimd.dma_start(out=trig[:, 0, :], in_=cos.unsqueeze(1).to_broadcast([T, B, HALF]))
         nc.gpsimd.dma_start(out=trig[:, 1, :], in_=sin.unsqueeze(1).to_broadcast([T, B, HALF]))
         ones = keep.tile([P, P], BF16)
@@ -71,6 +81,13 @@ def tile_multiheadattention_pa_s_kernel(tc, q_input, Wq_words, Wq_scales, q_scal
         nc.vector.memset(one[:], 1.0)
         unused = keep.tile([P, 1], F32)
         nc.scalar.activation(out=unused[:], in_=one[:], func=ACT.Abs_reciprocal_sqrt)
+
+        if WARM:
+            warm_src = keep.tile([P, max(WARM_N, P)], F32)
+            nc.vector.memset(warm_src[:], 0.0)
+            warm_ps = psum.tile([P, WARM_N], F32, tag="bank")
+            for i in range(WARM):
+                nc.tensor.matmul(out=warm_ps[:], lhsT=warm_src[:, 0:P], rhs=warm_src[:, 0:WARM_N], start=True, stop=True)
 
         x_words = x_sb[:].bitcast(F32)
         grouped = keep.tile([P, PASSES, 4 * P], BF16, align_bytes=64)
@@ -100,54 +117,77 @@ def tile_multiheadattention_pa_s_kernel(tc, q_input, Wq_words, Wq_scales, q_scal
             in1=gain[:].unsqueeze(1).to_broadcast([P, 2, 2, HALF]),
             op=ALU.mult,
         )
+        if ONE_ADD:
+            nc.vector.tensor_scalar(
+                out=tables[:, 1, 1, :], in0=tables[:, 1, 1, :], scalar1=-1.0, scalar2=0.0, op0=ALU.mult, op1=ALU.add
+            )
 
         squares = keep.tile([P, H, HD], F32)
         sumsq = keep.tile([P, H], F32)
         inv_rms = keep.tile([P, H], F32)
-        prods = keep.tile([P, H, 2, HD], F32)
-        o_sb = keep.tile([P, H, HD], F32)
-        for c in range(CHUNKS):
-            for i in range(BANKS_CHUNK):
-                first = HEADS_CHUNK * c + HEADS_BANK * i
-                acc = psum.tile([P, HEADS_BANK, HD], F32, name="acc%d" % first, tag="bank")
-                for j in range(HEADS_BANK):
-                    h = first + j
-                    for g in range(PASSES):
-                        nc.tensor.matmul_mx(
-                            out=acc[:, j, :],
-                            lhsT=x_codes[:, g, :].bitcast(FP8X4),
-                            lhsT_scale=x_scales[:, g, :],
-                            rhs=w_words[:, g, 2 * HD * h : 2 * HD * (h + 1)].bitcast(FP4X4),
-                            rhs_scale=w_scales[:, g, HD * h : HD * (h + 1)],
-                            start=(g == 0),
-                            stop=(g == PASSES - 1),
-                        )
-                for j in range(HEADS_BANK):
-                    h = first + j
-                    nc.scalar.activation(
-                        out=squares[:, h, :], in_=acc[:, j, :], func=ACT.Square, accum_out=sumsq[:, h : h + 1]
-                    )
-                pair = slice(first, first + HEADS_BANK)
-                nc.scalar.activation(
-                    out=inv_rms[:, pair], in_=sumsq[:, pair], func=ACT.Abs_reciprocal_sqrt, scale=1.0 / HD, bias=EPS
+        prods = keep.tile([P, H, 2, 2, HALF], F32)
+        o_sb = keep.tile([P, H, 2, HALF], F32)
+        group_end = {}
+        for lo, hi, eng in GROUPS:
+            group_end[hi] = (lo, eng)
+
+        def add_and_store(lo, hi, eng):
+            adder = nc.gpsimd if eng == "g" else nc.vector
+            heads = slice(lo, hi)
+            if ONE_ADD:
+                adder.tensor_tensor(
+                    out=o_sb[:, heads, :, :], in0=prods[:, heads, 0, :, :], in1=prods[:, heads, 1, ::-1, :], op=ALU.add
                 )
-                for j in range(HEADS_BANK):
-                    h = first + j
-                    nc.vector.scalar_tensor_tensor(
-                        out=prods[:, h, :, :],
-                        in0=acc[:, j, :].unsqueeze(1).to_broadcast([P, 2, HD]),
-                        scalar=inv_rms[:, h : h + 1],
-                        in1=tables[:].rearrange("p s f j -> p s (f j)"),
-                        op0=ALU.mult,
-                        op1=ALU.mult,
+            else:
+                adder.tensor_tensor(
+                    out=o_sb[:, heads, 0, :], in0=prods[:, heads, 0, 0, :], in1=prods[:, heads, 1, 1, :], op=ALU.subtract
+                )
+                adder.tensor_tensor(
+                    out=o_sb[:, heads, 1, :], in0=prods[:, heads, 0, 1, :], in1=prods[:, heads, 1, 0, :], op=ALU.add
+                )
+            if hi - lo == 1:
+                nc.sync.dma_start(
+                    out=out[:, lo, :, :].rearrange("b t d -> t b d"), in_=o_sb[:, lo, :, :].rearrange("p f j -> p (f j)")
+                )
+            else:
+                for b in range(B):
+                    nc.sync.dma_start(
+                        out=out[b, heads, :, :].rearrange("h t d -> t h d"),
+                        in_=o_sb[b:P:B, heads, :, :].rearrange("p h f j -> p h (f j)"),
                     )
-            adder = nc.gpsimd if c < CHUNKS - 1 else nc.vector
-            heads = slice(HEADS_CHUNK * c, HEADS_CHUNK * (c + 1))
-            adder.tensor_tensor(
-                out=o_sb[:, heads, 0:HALF], in0=prods[:, heads, 0, 0:HALF], in1=prods[:, heads, 1, HALF:HD], op=ALU.subtract
+
+        first = 0
+        for n_heads in BANKS:
+            acc = psum.tile([P, n_heads, HD], F32, name="acc%d" % first, tag="bank")
+            for j in range(n_heads):
+                h = first + j
+                for g in range(PASSES):
+                    nc.tensor.matmul_mx(
+                        out=acc[:, j, :],
+                        lhsT=x_codes[:, g, :].bitcast(FP8X4),
+                        lhsT_scale=x_scales[:, g, :],
+                        rhs=w_words[:, g, 2 * HD * h : 2 * HD * (h + 1)].bitcast(FP4X4),
+                        rhs_scale=w_scales[:, g, HD * h : HD * (h + 1)],
+                        start=(g == 0),
+                        stop=(g == PASSES - 1),
+                    )
+            for j in range(n_heads):
+                h = first + j
+                nc.scalar.activation(out=squares[:, h, :], in_=acc[:, j, :], func=ACT.Square, accum_out=sumsq[:, h : h + 1])
+            these = slice(first, first + n_heads)
+            nc.scalar.activation(
+                out=inv_rms[:, these], in_=sumsq[:, these], func=ACT.Abs_reciprocal_sqrt, scale=1.0 / HD, bias=EPS
             )
-            adder.tensor_tensor(
-                out=o_sb[:, heads, HALF:HD], in0=prods[:, heads, 0, HALF:HD], in1=prods[:, heads, 1, 0:HALF], op=ALU.add
-            )
-            for b in range(B):
-                nc.sync.dma_start(out=out[b, heads, :, :].rearrange("h t d -> t h d"), in_=o_sb[b:P:B, heads, :])
+            for j in range(n_heads):
+                h = first + j
+                nc.vector.scalar_tensor_tensor(
+                    out=prods[:, h, :, :, :].rearrange("p s f j -> p s (f j)"),
+                    in0=acc[:, j, :].unsqueeze(1).to_broadcast([P, 2, HD]),
+                    scalar=inv_rms[:, h : h + 1],
+                    in1=tables[:].rearrange("p s f j -> p s (f j)"),
+                    op0=ALU.mult,
+                    op1=ALU.mult,
+                )
+                if h + 1 in group_end:
+                    add_and_store(group_end[h + 1][0], h + 1, group_end[h + 1][1])
+            first += n_heads

@@ -23,11 +23,11 @@ N_OUT = H * HD
 HEADS_CHUNK = 4
 CHUNKS = H // HEADS_CHUNK
 
-BANKS = [2,2,2,2,2,2,2,2]
+W_CHUNKS = [[0,4],[4,8],[8,12],[12,16]]
+TILES = [[0,2,2],[2,2,3],[4,2,4],[6,2,5],[8,2,6],[10,2,7],[12,2,0],[14,2,1]]
+LATE = 0
+LATE_AFTER = 14
 GROUPS = [[0,2,'g'],[2,5,'g'],[5,8,'g'],[8,11,'g'],[11,13,'g'],[13,16,'v']]
-ONE_ADD = True
-WARM = 0
-WARM_N = 128
 
 FLOPS = 2 * B * T * D * N_OUT
 
@@ -36,13 +36,19 @@ def tile_multiheadattention_pa_s_kernel(tc, q_input, Wq_words, Wq_scales, q_scal
     nc = tc.nc
     with ExitStack() as ctx:
         keep = ctx.enter_context(tc.tile_pool(name="keep", bufs=1))
-        psum = ctx.enter_context(tc.psum_pool(name="psum", bufs=8))
+        psum = ctx.enter_context(tc.psum_pool(name="psum", bufs=1))
         ctx.enter_context(tc.manual_schedule())
 
         q_scale_row = keep.tile([P, HD], BF16)
         x_sb = keep.tile([P, D], BF16)
         w_scales = keep.tile([P, PASSES, N_OUT], U8, align_bytes=64)
-        w_words = keep.tile([P, PASSES, 2 * N_OUT], U8, align_bytes=64)
+        w_words = {}
+        w_first = {}
+        for lo, hi in W_CHUNKS:
+            chunk = keep.tile([P, PASSES, 2 * HD * (hi - lo)], U8, name="w_words%d" % lo, align_bytes=64)
+            for h in range(lo, hi):
+                w_words[h] = chunk
+                w_first[h] = lo
         trig = keep.tile([P, 2, HALF], BF16)
         ident = keep.tile([P, P], F32)
         planes_i32 = w_scales[:].bitcast(I32)
@@ -59,21 +65,22 @@ def tile_multiheadattention_pa_s_kernel(tc, q_input, Wq_words, Wq_scales, q_scal
         def load_words(lo, hi):
             w_bytes = slice(2 * HD * lo, 2 * HD * hi)
             nc.sync.dma_start(
-                out=w_words[:, :, w_bytes].bitcast(I32),
+                out=w_words[lo][:].bitcast(I32),
                 in_=Wq_words[:, :, w_bytes].bitcast(I32).rearrange("g p n -> p g n"),
             )
 
-        nc.vector.memset(q_scale_row[:], 0.0)
-        nc.scalar.dma_start(out=q_scale_row[0:1, :], in_=q_scale.unsqueeze(0))
+        nc.gpsimd.memset(q_scale_row[:], 0.0)
+        nc.gpsimd.dma_start(out=q_scale_row[0:1, :], in_=q_scale.unsqueeze(0))
+        make_identity(nc, ident[:])
+        nc.vector.memset(w_scales[:].bitcast(I32), 0)
+        nc.scalar.dma_start(out=trig[:, 0, :], in_=cos.unsqueeze(1).to_broadcast([T, B, HALF]))
         for g in range(PASSES):
             load_x(nc.sync, g)
-        nc.vector.memset(w_scales[:].bitcast(I32), 0)
+        load_words(0, 4)
         load_scales()
-        for c in range(CHUNKS):
+        nc.sync.dma_start(out=trig[:, 1, :], in_=sin.unsqueeze(1).to_broadcast([T, B, HALF]))
+        for c in range(1, CHUNKS):
             load_words(HEADS_CHUNK * c, HEADS_CHUNK * (c + 1))
-        make_identity(nc, ident[:])
-        nc.gpsimd.dma_start(out=trig[:, 0, :], in_=cos.unsqueeze(1).to_broadcast([T, B, HALF]))
-        nc.gpsimd.dma_start(out=trig[:, 1, :], in_=sin.unsqueeze(1).to_broadcast([T, B, HALF]))
         ones = keep.tile([P, P], BF16)
         nc.vector.memset(ones[:], 1.0)
 
@@ -82,45 +89,40 @@ def tile_multiheadattention_pa_s_kernel(tc, q_input, Wq_words, Wq_scales, q_scal
         unused = keep.tile([P, 1], F32)
         nc.scalar.activation(out=unused[:], in_=one[:], func=ACT.Abs_reciprocal_sqrt)
 
-        if WARM:
-            warm_src = keep.tile([P, max(WARM_N, P)], F32)
-            nc.vector.memset(warm_src[:], 0.0)
-            warm_ps = psum.tile([P, WARM_N], F32, tag="bank")
-            for i in range(WARM):
-                nc.tensor.matmul(out=warm_ps[:], lhsT=warm_src[:, 0:P], rhs=warm_src[:, 0:WARM_N], start=True, stop=True)
-
         x_words = x_sb[:].bitcast(F32)
         grouped = keep.tile([P, PASSES, 4 * P], BF16, align_bytes=64)
         x_codes = keep.tile([P, PASSES, P], U32, align_bytes=64)
         x_scales = keep.tile([P, PASSES, P], U8, align_bytes=64)
         copy_out = [nc.vector.tensor_copy, nc.scalar.copy]
+        front = [
+            psum.tile([P, 3, P], F32, name="front0", tag="bank0"),
+            psum.tile([P, 2, P], F32, name="front1", tag="bank1"),
+        ]
         for g in range(PASSES):
-            xT = psum.tile([P, 2, P], F32, name="xT%d" % g, tag="bank")
+            xT = front[g]
             for u in range(2):
                 nc.tensor.transpose(xT[:, u, :], x_words[:, 256 * g + u : 256 * (g + 1) : 2], ident[:])
             copy_out[g](
                 out=grouped[:, g, :].bitcast(F32).rearrange("p (m u) -> p m u", u=2),
-                in_=xT[:].rearrange("p u m -> p m u"),
+                in_=xT[:, 0:2, :].rearrange("p u m -> p m u"),
             )
             nc.vector.quantize_mx(out=x_codes[:, g, :].bitcast(FP8X4), scales=x_scales[:, g, :], in_=grouped[:, g, :])
 
-        q_scale_ps = psum.tile([P, HD], F32, tag="bank")
-        nc.tensor.matmul(out=q_scale_ps[:], lhsT=ones[:], rhs=q_scale_row[:], start=True, stop=True)
+        q_scale_ps = front[0][:, 2, :]
+        nc.tensor.matmul(out=q_scale_ps, lhsT=ones[:], rhs=q_scale_row[:], start=True, stop=True)
         gain = keep.tile([P, 2, HALF], F32)
         nc.vector.tensor_scalar(
-            out=gain[:].rearrange("p f j -> p (f j)"), in0=q_scale_ps[:], scalar1=1.0, scalar2=1.0, op0=ALU.mult, op1=ALU.add
+            out=gain[:].rearrange("p f j -> p (f j)"), in0=q_scale_ps, scalar1=1.0, scalar2=1.0, op0=ALU.mult, op1=ALU.add
         )
         tables = keep.tile([P, 2, 2, HALF], F32)
         nc.vector.tensor_tensor(
-            out=tables[:],
-            in0=trig[:].unsqueeze(2).to_broadcast([P, 2, 2, HALF]),
-            in1=gain[:].unsqueeze(1).to_broadcast([P, 2, 2, HALF]),
-            op=ALU.mult,
+            out=tables[:, 0, :, :], in0=trig[:, 0, :].unsqueeze(1).to_broadcast([P, 2, HALF]), in1=gain[:], op=ALU.mult
         )
-        if ONE_ADD:
-            nc.vector.tensor_scalar(
-                out=tables[:, 1, 1, :], in0=tables[:, 1, 1, :], scalar1=-1.0, scalar2=0.0, op0=ALU.mult, op1=ALU.add
-            )
+        nc.vector.tensor_tensor(out=tables[:, 1, 0, :], in0=trig[:, 1, :], in1=gain[:, 0, :], op=ALU.mult)
+        nc.vector.scalar_tensor_tensor(
+            out=tables[:, 1, 1, :], in0=trig[:, 1, :], scalar=-1.0, in1=gain[:, 1, :], op0=ALU.mult, op1=ALU.mult
+        )
+        tables_flat = tables[:].rearrange("p s f j -> p s (f j)")
 
         squares = keep.tile([P, H, HD], F32)
         sumsq = keep.tile([P, H], F32)
@@ -131,20 +133,8 @@ def tile_multiheadattention_pa_s_kernel(tc, q_input, Wq_words, Wq_scales, q_scal
         for lo, hi, eng in GROUPS:
             group_end[hi] = (lo, eng)
 
-        def add_and_store(lo, hi, eng):
-            adder = nc.gpsimd if eng == "g" else nc.vector
+        def store(lo, hi):
             heads = slice(lo, hi)
-            if ONE_ADD:
-                adder.tensor_tensor(
-                    out=o_sb[:, heads, :, :], in0=prods[:, heads, 0, :, :], in1=prods[:, heads, 1, ::-1, :], op=ALU.add
-                )
-            else:
-                adder.tensor_tensor(
-                    out=o_sb[:, heads, 0, :], in0=prods[:, heads, 0, 0, :], in1=prods[:, heads, 1, 1, :], op=ALU.subtract
-                )
-                adder.tensor_tensor(
-                    out=o_sb[:, heads, 1, :], in0=prods[:, heads, 0, 1, :], in1=prods[:, heads, 1, 0, :], op=ALU.add
-                )
             if hi - lo == 1:
                 nc.sync.dma_start(
                     out=out[:, lo, :, :].rearrange("b t d -> t b d"), in_=o_sb[:, lo, :, :].rearrange("p f j -> p (f j)")
@@ -156,21 +146,14 @@ def tile_multiheadattention_pa_s_kernel(tc, q_input, Wq_words, Wq_scales, q_scal
                         in_=o_sb[b:P:B, heads, :, :].rearrange("p h f j -> p h (f j)"),
                     )
 
-        first = 0
-        for n_heads in BANKS:
-            acc = psum.tile([P, n_heads, HD], F32, name="acc%d" % first, tag="bank")
-            for j in range(n_heads):
-                h = first + j
-                for g in range(PASSES):
-                    nc.tensor.matmul_mx(
-                        out=acc[:, j, :],
-                        lhsT=x_codes[:, g, :].bitcast(FP8X4),
-                        lhsT_scale=x_scales[:, g, :],
-                        rhs=w_words[:, g, 2 * HD * h : 2 * HD * (h + 1)].bitcast(FP4X4),
-                        rhs_scale=w_scales[:, g, HD * h : HD * (h + 1)],
-                        start=(g == 0),
-                        stop=(g == PASSES - 1),
-                    )
+        def add(lo, hi, eng):
+            adder = nc.gpsimd if eng == "g" else nc.vector
+            heads = slice(lo, hi)
+            adder.tensor_tensor(
+                out=o_sb[:, heads, :, :], in0=prods[:, heads, 0, :, :], in1=prods[:, heads, 1, ::-1, :], op=ALU.add
+            )
+
+        def squares_and_root(acc, first, n_heads):
             for j in range(n_heads):
                 h = first + j
                 nc.scalar.activation(out=squares[:, h, :], in_=acc[:, j, :], func=ACT.Square, accum_out=sumsq[:, h : h + 1])
@@ -178,16 +161,50 @@ def tile_multiheadattention_pa_s_kernel(tc, q_input, Wq_words, Wq_scales, q_scal
             nc.scalar.activation(
                 out=inv_rms[:, these], in_=sumsq[:, these], func=ACT.Abs_reciprocal_sqrt, scale=1.0 / HD, bias=EPS
             )
+
+        late_acc = None
+        for first, n_heads, bank in TILES:
+            acc = psum.tile([P, n_heads, HD], F32, name="acc%d" % first, tag="bank%d" % bank)
+            for j in range(n_heads):
+                h = first + j
+                for g in range(PASSES):
+                    nc.tensor.matmul_mx(
+                        out=acc[:, j, :],
+                        lhsT=x_codes[:, g, :].bitcast(FP8X4),
+                        lhsT_scale=x_scales[:, g, :],
+                        rhs=w_words[h][:, g, 2 * HD * (h - w_first[h]) : 2 * HD * (h - w_first[h] + 1)].bitcast(FP4X4),
+                        rhs_scale=w_scales[:, g, HD * h : HD * (h + 1)],
+                        start=(g == 0),
+                        stop=(g == PASSES - 1),
+                    )
+            if first < LATE:
+                late_acc = acc
+                nc.vector.tensor_tensor(
+                    out=prods[:, first : first + n_heads, :, :, :].rearrange("p h s f j -> p h s (f j)"),
+                    in0=acc[:].unsqueeze(2).to_broadcast([P, n_heads, 2, HD]),
+                    in1=tables_flat.unsqueeze(1).to_broadcast([P, n_heads, 2, HD]),
+                    op=ALU.mult,
+                )
+                add(first, first + n_heads, "g")
+                continue
+            squares_and_root(acc, first, n_heads)
+            if LATE and first == LATE_AFTER:
+                squares_and_root(late_acc, 0, LATE)
+                for h in range(LATE):
+                    nc.scalar.activation(
+                        out=o_sb[:, h, :, :], in_=o_sb[:, h, :, :], func=ACT.Copy, scale=inv_rms[:, h : h + 1]
+                    )
+                store(0, LATE)
             for j in range(n_heads):
                 h = first + j
                 nc.vector.scalar_tensor_tensor(
                     out=prods[:, h, :, :, :].rearrange("p s f j -> p s (f j)"),
                     in0=acc[:, j, :].unsqueeze(1).to_broadcast([P, 2, HD]),
                     scalar=inv_rms[:, h : h + 1],
-                    in1=tables[:].rearrange("p s f j -> p s (f j)"),
+                    in1=tables_flat,
                     op0=ALU.mult,
                     op1=ALU.mult,
                 )
                 if h + 1 in group_end:
-                    add_and_store(group_end[h + 1][0], h + 1, group_end[h + 1][1])
-            first += n_heads
+                    add(group_end[h + 1][0], h + 1, group_end[h + 1][1])
+                    store(group_end[h + 1][0], h + 1)

@@ -22,12 +22,12 @@ PASSES = D // K_PASS
 N_OUT = H * HD
 HEADS_CHUNK = 4
 CHUNKS = H // HEADS_CHUNK
+PAIRS = H // 2
 
 W_CHUNKS = [[0,4],[4,8],[8,12],[12,16]]
-TILES = [[0,2,2],[2,2,3],[4,2,4],[6,2,5],[8,2,6],[10,2,7],[12,2,0],[14,2,1]]
-LATE = 0
-LATE_AFTER = 14
+BANK_OF_PAIR = [2,3,4,5,6,7,0,1]
 GROUPS = [[0,2,'g'],[2,5,'g'],[5,8,'g'],[8,11,'g'],[11,13,'g'],[13,16,'v']]
+AHEAD = 1
 
 FLOPS = 2 * B * T * D * N_OUT
 
@@ -69,13 +69,13 @@ def tile_multiheadattention_pa_s_kernel(tc, q_input, Wq_words, Wq_scales, q_scal
                 in_=Wq_words[:, :, w_bytes].bitcast(I32).rearrange("g p n -> p g n"),
             )
 
-        nc.gpsimd.memset(q_scale_row[:], 0.0)
-        nc.gpsimd.dma_start(out=q_scale_row[0:1, :], in_=q_scale.unsqueeze(0))
+        nc.gpsimd.dma_start(out=trig[:, 0, :], in_=cos.unsqueeze(1).to_broadcast([T, B, HALF]))
         make_identity(nc, ident[:])
+        nc.vector.memset(q_scale_row[:], 0.0)
         nc.vector.memset(w_scales[:].bitcast(I32), 0)
-        nc.scalar.dma_start(out=trig[:, 0, :], in_=cos.unsqueeze(1).to_broadcast([T, B, HALF]))
         for g in range(PASSES):
             load_x(nc.sync, g)
+        nc.scalar.dma_start(out=q_scale_row[0:1, :], in_=q_scale.unsqueeze(0))
         load_words(0, 4)
         load_scales()
         nc.sync.dma_start(out=trig[:, 1, :], in_=sin.unsqueeze(1).to_broadcast([T, B, HALF]))
@@ -132,6 +132,34 @@ def tile_multiheadattention_pa_s_kernel(tc, q_input, Wq_words, Wq_scales, q_scal
         group_end = {}
         for lo, hi, eng in GROUPS:
             group_end[hi] = (lo, eng)
+        acc_of = {}
+
+        def passes(pair):
+            acc = psum.tile([P, 2, HD], F32, name="acc%d" % pair, tag="bank%d" % BANK_OF_PAIR[pair])
+            acc_of[pair] = acc
+            for j in range(2):
+                h = 2 * pair + j
+                for g in range(PASSES):
+                    nc.tensor.matmul_mx(
+                        out=acc[:, j, :],
+                        lhsT=x_codes[:, g, :].bitcast(FP8X4),
+                        lhsT_scale=x_scales[:, g, :],
+                        rhs=w_words[h][:, g, 2 * HD * (h - w_first[h]) : 2 * HD * (h - w_first[h] + 1)].bitcast(FP4X4),
+                        rhs_scale=w_scales[:, g, HD * h : HD * (h + 1)],
+                        start=(g == 0),
+                        stop=(g == PASSES - 1),
+                    )
+
+        def square(h):
+            nc.scalar.activation(
+                out=squares[:, h, :], in_=acc_of[h // 2][:, h % 2, :], func=ACT.Square, accum_out=sumsq[:, h : h + 1]
+            )
+
+        def root(pair):
+            these = slice(2 * pair, 2 * pair + 2)
+            nc.scalar.activation(
+                out=inv_rms[:, these], in_=sumsq[:, these], func=ACT.Abs_reciprocal_sqrt, scale=1.0 / HD, bias=EPS
+            )
 
         def store(lo, hi):
             heads = slice(lo, hi)
@@ -146,65 +174,41 @@ def tile_multiheadattention_pa_s_kernel(tc, q_input, Wq_words, Wq_scales, q_scal
                         in_=o_sb[b:P:B, heads, :, :].rearrange("p h f j -> p h (f j)"),
                     )
 
-        def add(lo, hi, eng):
-            adder = nc.gpsimd if eng == "g" else nc.vector
-            heads = slice(lo, hi)
-            adder.tensor_tensor(
-                out=o_sb[:, heads, :, :], in0=prods[:, heads, 0, :, :], in1=prods[:, heads, 1, ::-1, :], op=ALU.add
-            )
-
-        def squares_and_root(acc, first, n_heads):
-            for j in range(n_heads):
-                h = first + j
-                nc.scalar.activation(out=squares[:, h, :], in_=acc[:, j, :], func=ACT.Square, accum_out=sumsq[:, h : h + 1])
-            these = slice(first, first + n_heads)
-            nc.scalar.activation(
-                out=inv_rms[:, these], in_=sumsq[:, these], func=ACT.Abs_reciprocal_sqrt, scale=1.0 / HD, bias=EPS
-            )
-
-        late_acc = None
-        for first, n_heads, bank in TILES:
-            acc = psum.tile([P, n_heads, HD], F32, name="acc%d" % first, tag="bank%d" % bank)
-            for j in range(n_heads):
-                h = first + j
-                for g in range(PASSES):
-                    nc.tensor.matmul_mx(
-                        out=acc[:, j, :],
-                        lhsT=x_codes[:, g, :].bitcast(FP8X4),
-                        lhsT_scale=x_scales[:, g, :],
-                        rhs=w_words[h][:, g, 2 * HD * (h - w_first[h]) : 2 * HD * (h - w_first[h] + 1)].bitcast(FP4X4),
-                        rhs_scale=w_scales[:, g, HD * h : HD * (h + 1)],
-                        start=(g == 0),
-                        stop=(g == PASSES - 1),
-                    )
-            if first < LATE:
-                late_acc = acc
-                nc.vector.tensor_tensor(
-                    out=prods[:, first : first + n_heads, :, :, :].rearrange("p h s f j -> p h s (f j)"),
-                    in0=acc[:].unsqueeze(2).to_broadcast([P, n_heads, 2, HD]),
-                    in1=tables_flat.unsqueeze(1).to_broadcast([P, n_heads, 2, HD]),
-                    op=ALU.mult,
-                )
-                add(first, first + n_heads, "g")
-                continue
-            squares_and_root(acc, first, n_heads)
-            if LATE and first == LATE_AFTER:
-                squares_and_root(late_acc, 0, LATE)
-                for h in range(LATE):
-                    nc.scalar.activation(
-                        out=o_sb[:, h, :, :], in_=o_sb[:, h, :, :], func=ACT.Copy, scale=inv_rms[:, h : h + 1]
-                    )
-                store(0, LATE)
-            for j in range(n_heads):
-                h = first + j
+        def products(pair):
+            for h in (2 * pair, 2 * pair + 1):
                 nc.vector.scalar_tensor_tensor(
                     out=prods[:, h, :, :, :].rearrange("p s f j -> p s (f j)"),
-                    in0=acc[:, j, :].unsqueeze(1).to_broadcast([P, 2, HD]),
+                    in0=acc_of[pair][:, h % 2, :].unsqueeze(1).to_broadcast([P, 2, HD]),
                     scalar=inv_rms[:, h : h + 1],
                     in1=tables_flat,
                     op0=ALU.mult,
                     op1=ALU.mult,
                 )
                 if h + 1 in group_end:
-                    add(group_end[h + 1][0], h + 1, group_end[h + 1][1])
-                    store(group_end[h + 1][0], h + 1)
+                    lo, eng = group_end[h + 1]
+                    adder = nc.gpsimd if eng == "g" else nc.vector
+                    adder.tensor_tensor(
+                        out=o_sb[:, lo : h + 1, :, :],
+                        in0=prods[:, lo : h + 1, 0, :, :],
+                        in1=prods[:, lo : h + 1, 1, ::-1, :],
+                        op=ALU.add,
+                    )
+                    store(lo, h + 1)
+
+        passes(0)
+        square(0)
+        square(1)
+        root(0)
+        products(0)
+        squared = 2
+        issued = 1
+        for pair in range(1, PAIRS):
+            upto = min(H, 2 * pair + 2 + AHEAD)
+            while squared < upto:
+                if squared // 2 >= issued:
+                    passes(issued)
+                    issued += 1
+                square(squared)
+                squared += 1
+            root(pair)
+            products(pair)

@@ -20,11 +20,10 @@ P = 128
 K_PASS = 512
 PASSES = D // K_PASS
 N_OUT = H * HD
-HEADS_CHUNK = 4
-CHUNKS = H // HEADS_CHUNK
 PAIRS = H // 2
 
 W_CHUNKS = [[0,4],[4,8],[8,12],[12,16]]
+SCALE_HEADS = 8
 BANK_OF_PAIR = [2,3,4,5,6,7,0,1]
 GROUPS = [[0,2,'g'],[2,5,'g'],[5,8,'g'],[8,11,'g'],[11,13,'g'],[13,16,'v']]
 AHEAD = 1
@@ -41,7 +40,10 @@ def tile_multiheadattention_pa_s_kernel(tc, q_input, Wq_words, Wq_scales, q_scal
 
         q_scale_row = keep.tile([P, HD], BF16)
         x_sb = keep.tile([P, D], BF16)
-        w_scales = keep.tile([P, PASSES, N_OUT], U8, align_bytes=64)
+        w_scales = [
+            keep.tile([P, PASSES, HD * SCALE_HEADS], U8, name="w_scales%d" % s, align_bytes=64)
+            for s in range(H // SCALE_HEADS)
+        ]
         w_words = {}
         w_first = {}
         for lo, hi in W_CHUNKS:
@@ -51,16 +53,18 @@ def tile_multiheadattention_pa_s_kernel(tc, q_input, Wq_words, Wq_scales, q_scal
                 w_first[h] = lo
         trig = keep.tile([P, 2, HALF], BF16)
         ident = keep.tile([P, P], F32)
-        planes_i32 = w_scales[:].bitcast(I32)
-        scales_i32 = Wq_scales.bitcast(I32)
 
         def load_x(queue, g):
             k_cols = slice(K_PASS * g, K_PASS * (g + 1))
             queue.dma_start(out=x_sb[:, k_cols], in_=q_input[:, :, k_cols].rearrange("b t k -> t b k"))
 
-        def load_scales():
+        def load_scales(s):
+            n_cols = slice(HD * SCALE_HEADS * s, HD * SCALE_HEADS * (s + 1))
             for r in range(4):
-                nc.sync.dma_start(out=planes_i32[r:P:32], in_=scales_i32[:, r:16:4, :].rearrange("g q n -> q g n"))
+                nc.sync.dma_start(
+                    out=w_scales[s][:].bitcast(I32)[r:P:32],
+                    in_=Wq_scales[:, r:16:4, n_cols].bitcast(I32).rearrange("g q n -> q g n"),
+                )
 
         def load_words(lo, hi):
             w_bytes = slice(2 * HD * lo, 2 * HD * hi)
@@ -71,23 +75,29 @@ def tile_multiheadattention_pa_s_kernel(tc, q_input, Wq_words, Wq_scales, q_scal
 
         nc.gpsimd.dma_start(out=trig[:, 0, :], in_=cos.unsqueeze(1).to_broadcast([T, B, HALF]))
         make_identity(nc, ident[:])
-        nc.vector.memset(q_scale_row[:], 0.0)
-        nc.vector.memset(w_scales[:].bitcast(I32), 0)
-        for g in range(PASSES):
-            load_x(nc.sync, g)
-        nc.scalar.dma_start(out=q_scale_row[0:1, :], in_=q_scale.unsqueeze(0))
-        load_words(0, 4)
-        load_scales()
-        nc.sync.dma_start(out=trig[:, 1, :], in_=sin.unsqueeze(1).to_broadcast([T, B, HALF]))
-        for c in range(1, CHUNKS):
-            load_words(HEADS_CHUNK * c, HEADS_CHUNK * (c + 1))
-        ones = keep.tile([P, P], BF16)
-        nc.vector.memset(ones[:], 1.0)
-
         one = keep.tile([P, 1], F32)
         nc.vector.memset(one[:], 1.0)
+        nc.vector.memset(w_scales[0][:].bitcast(I32), 0)
+        load_x(nc.sync, 0)
+        load_x(nc.scalar, 1)
+        load_words(0, 4)
+        load_scales(0)
+        nc.vector.memset(q_scale_row[:], 0.0)
+        nc.sync.dma_start(out=q_scale_row[0:1, :], in_=q_scale.unsqueeze(0))
+        ones = keep.tile([P, P], BF16)
+        nc.vector.memset(ones[:], 1.0)
+        neg_ones = keep.tile([P, P], BF16)
+        nc.vector.memset(neg_ones[:], -1.0)
+        nc.vector.memset(w_scales[1][:].bitcast(I32), 0)
+
         unused = keep.tile([P, 1], F32)
         nc.scalar.activation(out=unused[:], in_=one[:], func=ACT.Abs_reciprocal_sqrt)
+
+        nc.sync.dma_start(out=trig[:, 1, :], in_=sin.unsqueeze(1).to_broadcast([T, B, HALF]))
+        load_words(4, 8)
+        load_scales(1)
+        load_words(8, 12)
+        load_words(12, 16)
 
         x_words = x_sb[:].bitcast(F32)
         grouped = keep.tile([P, PASSES, 4 * P], BF16, align_bytes=64)
@@ -95,7 +105,7 @@ def tile_multiheadattention_pa_s_kernel(tc, q_input, Wq_words, Wq_scales, q_scal
         x_scales = keep.tile([P, PASSES, P], U8, align_bytes=64)
         copy_out = [nc.vector.tensor_copy, nc.scalar.copy]
         front = [
-            psum.tile([P, 3, P], F32, name="front0", tag="bank0"),
+            psum.tile([P, 2, P], F32, name="front0", tag="bank0"),
             psum.tile([P, 2, P], F32, name="front1", tag="bank1"),
         ]
         for g in range(PASSES):
@@ -104,25 +114,9 @@ def tile_multiheadattention_pa_s_kernel(tc, q_input, Wq_words, Wq_scales, q_scal
                 nc.tensor.transpose(xT[:, u, :], x_words[:, 256 * g + u : 256 * (g + 1) : 2], ident[:])
             copy_out[g](
                 out=grouped[:, g, :].bitcast(F32).rearrange("p (m u) -> p m u", u=2),
-                in_=xT[:, 0:2, :].rearrange("p u m -> p m u"),
+                in_=xT[:].rearrange("p u m -> p m u"),
             )
             nc.vector.quantize_mx(out=x_codes[:, g, :].bitcast(FP8X4), scales=x_scales[:, g, :], in_=grouped[:, g, :])
-
-        q_scale_ps = front[0][:, 2, :]
-        nc.tensor.matmul(out=q_scale_ps, lhsT=ones[:], rhs=q_scale_row[:], start=True, stop=True)
-        gain = keep.tile([P, 2, HALF], F32)
-        nc.vector.tensor_scalar(
-            out=gain[:].rearrange("p f j -> p (f j)"), in0=q_scale_ps, scalar1=1.0, scalar2=1.0, op0=ALU.mult, op1=ALU.add
-        )
-        tables = keep.tile([P, 2, 2, HALF], F32)
-        nc.vector.tensor_tensor(
-            out=tables[:, 0, :, :], in0=trig[:, 0, :].unsqueeze(1).to_broadcast([P, 2, HALF]), in1=gain[:], op=ALU.mult
-        )
-        nc.vector.tensor_tensor(out=tables[:, 1, 0, :], in0=trig[:, 1, :], in1=gain[:, 0, :], op=ALU.mult)
-        nc.vector.scalar_tensor_tensor(
-            out=tables[:, 1, 1, :], in0=trig[:, 1, :], scalar=-1.0, in1=gain[:, 1, :], op0=ALU.mult, op1=ALU.mult
-        )
-        tables_flat = tables[:].rearrange("p s f j -> p s (f j)")
 
         squares = keep.tile([P, H, HD], F32)
         sumsq = keep.tile([P, H], F32)
@@ -145,7 +139,9 @@ def tile_multiheadattention_pa_s_kernel(tc, q_input, Wq_words, Wq_scales, q_scal
                         lhsT=x_codes[:, g, :].bitcast(FP8X4),
                         lhsT_scale=x_scales[:, g, :],
                         rhs=w_words[h][:, g, 2 * HD * (h - w_first[h]) : 2 * HD * (h - w_first[h] + 1)].bitcast(FP4X4),
-                        rhs_scale=w_scales[:, g, HD * h : HD * (h + 1)],
+                        rhs_scale=w_scales[h // SCALE_HEADS][
+                            :, g, HD * (h % SCALE_HEADS) : HD * (h % SCALE_HEADS + 1)
+                        ],
                         start=(g == 0),
                         stop=(g == PASSES - 1),
                     )
@@ -194,6 +190,28 @@ def tile_multiheadattention_pa_s_kernel(tc, q_input, Wq_words, Wq_scales, q_scal
                         op=ALU.add,
                     )
                     store(lo, h + 1)
+
+        spread = psum.tile([P, HD + HALF], F32, name="spread", tag="bank7")
+        q_scale_ps = spread[:, 0:HD]
+        nc.tensor.matmul(out=q_scale_ps, lhsT=ones[:], rhs=q_scale_row[:], start=True, stop=True)
+        neg_ps = spread[:, HD : HD + HALF]
+        nc.tensor.matmul(out=neg_ps, lhsT=neg_ones[:], rhs=q_scale_row[:, HALF:HD], start=True, stop=True)
+        tables = keep.tile([P, 2, 2, HALF], F32)
+        nc.vector.scalar_tensor_tensor(
+            out=tables[:, 0, :, :],
+            in0=q_scale_ps.rearrange("p (f j) -> p f j", f=2),
+            scalar=1.0,
+            in1=trig[:, 0, :].unsqueeze(1).to_broadcast([P, 2, HALF]),
+            op0=ALU.add,
+            op1=ALU.mult,
+        )
+        nc.vector.scalar_tensor_tensor(
+            out=tables[:, 1, 0, :], in0=q_scale_ps[:, 0:HALF], scalar=1.0, in1=trig[:, 1, :], op0=ALU.add, op1=ALU.mult
+        )
+        nc.vector.scalar_tensor_tensor(
+            out=tables[:, 1, 1, :], in0=neg_ps, scalar=-1.0, in1=trig[:, 1, :], op0=ALU.add, op1=ALU.mult
+        )
+        tables_flat = tables[:].rearrange("p s f j -> p s (f j)")
 
         passes(0)
         square(0)

@@ -73,17 +73,16 @@ def tile_multiheadattention_pa_s_kernel(tc, q_input, Wq_words, Wq_scales, q_scal
                 in_=Wq_words[:, :, w_bytes].bitcast(I32).rearrange("g p n -> p g n"),
             )
 
-        nc.gpsimd.dma_start(out=trig[:, 0, :], in_=cos.unsqueeze(1).to_broadcast([T, B, HALF]))
         make_identity(nc, ident[:])
         one = keep.tile([P, 1], F32)
         nc.vector.memset(one[:], 1.0)
+        nc.vector.memset(q_scale_row[:], 0.0)
         nc.vector.memset(w_scales[0][:].bitcast(I32), 0)
         load_x(nc.sync, 0)
-        load_x(nc.scalar, 1)
+        load_x(nc.sync, 1)
+        nc.scalar.dma_start(out=q_scale_row[0:1, :], in_=q_scale.unsqueeze(0))
         load_words(0, 4)
         load_scales(0)
-        nc.vector.memset(q_scale_row[:], 0.0)
-        nc.sync.dma_start(out=q_scale_row[0:1, :], in_=q_scale.unsqueeze(0))
         ones = keep.tile([P, P], BF16)
         nc.vector.memset(ones[:], 1.0)
         neg_ones = keep.tile([P, P], BF16)
@@ -93,6 +92,7 @@ def tile_multiheadattention_pa_s_kernel(tc, q_input, Wq_words, Wq_scales, q_scal
         unused = keep.tile([P, 1], F32)
         nc.scalar.activation(out=unused[:], in_=one[:], func=ACT.Abs_reciprocal_sqrt)
 
+        nc.sync.dma_start(out=trig[:, 0, :], in_=cos.unsqueeze(1).to_broadcast([T, B, HALF]))
         nc.sync.dma_start(out=trig[:, 1, :], in_=sin.unsqueeze(1).to_broadcast([T, B, HALF]))
         load_words(4, 8)
         load_scales(1)
@@ -221,7 +221,7 @@ def tile_multiheadattention_pa_s_kernel(tc, q_input, Wq_words, Wq_scales, q_scal
         squared = 2
         issued = 1
         for pair in range(1, PAIRS):
-            upto = min(H, 2 * pair + 2 + AHEAD)
+            upto = min(H, 2 * pair + 2 + (AHEAD if pair > 1 else 0))
             while squared < upto:
                 if squared // 2 >= issued:
                     passes(issued)

@@ -77,6 +77,8 @@ def tile_multiheadattention_pa_s_kernel(tc, q_input, Wq_words, Wq_scales, q_scal
         one = keep.tile([P, 1], F32)
         nc.vector.memset(one[:], 1.0)
         nc.vector.memset(q_scale_row[:], 0.0)
+        zeros = keep.tile([P, P], F32)
+        nc.vector.memset(zeros[:], 0.0)
         nc.vector.memset(w_scales[0][:].bitcast(I32), 0)
         load_x(nc.sync, 0)
         load_x(nc.sync, 1)
@@ -98,6 +100,14 @@ def tile_multiheadattention_pa_s_kernel(tc, q_input, Wq_words, Wq_scales, q_scal
         load_scales(1)
         load_words(8, 12)
         load_words(12, 16)
+
+        warm = psum.tile([P, P], F32, name="warm", tag="bank6")
+
+        def dummy_matmuls(count):
+            for n in range(count):
+                nc.tensor.matmul(out=warm[:], lhsT=zeros[:], rhs=zeros[:], start=True, stop=True)
+
+        dummy_matmuls(4)
 
         x_words = x_sb[:].bitcast(F32)
         grouped = keep.tile([P, PASSES, 4 * P], BF16, align_bytes=64)
@@ -190,6 +200,8 @@ def tile_multiheadattention_pa_s_kernel(tc, q_input, Wq_words, Wq_scales, q_scal
                         op=ALU.add,
                     )
                     store(lo, h + 1)
+
+        dummy_matmuls(2)
 
         spread = psum.tile([P, HD + HALF], F32, name="spread", tag="bank7")
         q_scale_ps = spread[:, 0:HD]

@@ -54,10 +54,6 @@ def tile_multiheadattention_pa_s_kernel(tc, q_input, Wq_words, Wq_scales, q_scal
         trig = keep.tile([P, 2, HALF], BF16)
         ident = keep.tile([P, P], F32)
 
-        def load_x(queue, g):
-            k_cols = slice(K_PASS * g, K_PASS * (g + 1))
-            queue.dma_start(out=x_sb[:, k_cols], in_=q_input[:, :, k_cols].rearrange("b t k -> t b k"))
-
         def load_scales(s):
             n_cols = slice(HD * SCALE_HEADS * s, HD * SCALE_HEADS * (s + 1))
             for r in range(4):
@@ -74,32 +70,30 @@ def tile_multiheadattention_pa_s_kernel(tc, q_input, Wq_words, Wq_scales, q_scal
             )
 
         make_identity(nc, ident[:])
-        one = keep.tile([P, 1], F32)
-        nc.vector.memset(one[:], 1.0)
-        nc.vector.memset(q_scale_row[:], 0.0)
         zeros = keep.tile([P, P], F32)
         nc.vector.memset(zeros[:], 0.0)
+        one = keep.tile([P, 1], F32)
+        nc.vector.memset(one[:], 1.0)
         nc.vector.memset(w_scales[0][:].bitcast(I32), 0)
-        load_x(nc.sync, 0)
-        load_x(nc.sync, 1)
-        nc.scalar.dma_start(out=q_scale_row[0:1, :], in_=q_scale.unsqueeze(0))
+        nc.scalar.dma_start(out=trig[:, 0, :], in_=cos.unsqueeze(1).to_broadcast([T, B, HALF]))
+        nc.scalar.dma_start(out=trig[:, 1, :], in_=sin.unsqueeze(1).to_broadcast([T, B, HALF]))
+        nc.sync.dma_start(out=x_sb[:], in_=q_input.rearrange("b t k -> t b k"))
         load_words(0, 4)
         load_scales(0)
+        nc.vector.memset(q_scale_row[:], 0.0)
+        nc.sync.dma_start(out=q_scale_row[0:1, :], in_=q_scale.unsqueeze(0))
+        load_words(4, 8)
         ones = keep.tile([P, P], BF16)
         nc.vector.memset(ones[:], 1.0)
         neg_ones = keep.tile([P, P], BF16)
         nc.vector.memset(neg_ones[:], -1.0)
         nc.vector.memset(w_scales[1][:].bitcast(I32), 0)
-
-        unused = keep.tile([P, 1], F32)
-        nc.scalar.activation(out=unused[:], in_=one[:], func=ACT.Abs_reciprocal_sqrt)
-
-        nc.sync.dma_start(out=trig[:, 0, :], in_=cos.unsqueeze(1).to_broadcast([T, B, HALF]))
-        nc.sync.dma_start(out=trig[:, 1, :], in_=sin.unsqueeze(1).to_broadcast([T, B, HALF]))
-        load_words(4, 8)
         load_scales(1)
         load_words(8, 12)
         load_words(12, 16)
+
+        unused = keep.tile([P, 1], F32)
+        nc.scalar.activation(out=unused[:], in_=one[:], func=ACT.Abs_reciprocal_sqrt)
 
         warm = psum.tile([P, P], F32, name="warm", tag="bank6")
 
@@ -107,7 +101,7 @@ def tile_multiheadattention_pa_s_kernel(tc, q_input, Wq_words, Wq_scales, q_scal
             for n in range(count):
                 nc.tensor.matmul(out=warm[:], lhsT=zeros[:], rhs=zeros[:], start=True, stop=True)
 
-        dummy_matmuls(4)
+        dummy_matmuls(2)
 
         x_words = x_sb[:].bitcast(F32)
         grouped = keep.tile([P, PASSES, 4 * P], BF16, align_bytes=64)
@@ -201,7 +195,7 @@ def tile_multiheadattention_pa_s_kernel(tc, q_input, Wq_words, Wq_scales, q_scal
                     )
                     store(lo, h + 1)
 
-        dummy_matmuls(2)
+        passes(0)
 
         spread = psum.tile([P, HD + HALF], F32, name="spread", tag="bank7")
         q_scale_ps = spread[:, 0:HD]
@@ -225,7 +219,6 @@ def tile_multiheadattention_pa_s_kernel(tc, q_input, Wq_words, Wq_scales, q_scal
         )
         tables_flat = tables[:].rearrange("p s f j -> p s (f j)")
 
-        passes(0)
         square(0)
         square(1)
         root(0)

@@ -24,7 +24,8 @@ PAIRS = H // 2
 
 W_CHUNKS = [[0,4],[4,8],[8,12],[12,16]]
 SCALE_HEADS = 8
-BANK_OF_PAIR = [2,3,4,5,6,7,0,1]
+BANK_OF_PAIR = [2,4,5,6,7,0,1,2]
+BANK_OF_HEAD_1 = 3
 GROUPS = [[0,2,'g'],[2,5,'g'],[5,8,'g'],[8,11,'g'],[11,13,'g'],[13,16,'v']]
 AHEAD = 1
 
@@ -74,19 +75,22 @@ def tile_multiheadattention_pa_s_kernel(tc, q_input, Wq_words, Wq_scales, q_scal
         nc.vector.memset(zeros[:], 0.0)
         one = keep.tile([P, 1], F32)
         nc.vector.memset(one[:], 1.0)
+        nc.vector.memset(q_scale_row[:], 0.0)
         nc.vector.memset(w_scales[0][:].bitcast(I32), 0)
         nc.scalar.dma_start(out=trig[:, 0, :], in_=cos.unsqueeze(1).to_broadcast([T, B, HALF]))
-        nc.scalar.dma_start(out=trig[:, 1, :], in_=sin.unsqueeze(1).to_broadcast([T, B, HALF]))
+        nc.scalar.dma_start(out=q_scale_row[0:1, :], in_=q_scale.unsqueeze(0))
         nc.sync.dma_start(out=x_sb[:], in_=q_input.rearrange("b t k -> t b k"))
         load_words(0, 4)
         load_scales(0)
-        nc.vector.memset(q_scale_row[:], 0.0)
-        nc.sync.dma_start(out=q_scale_row[0:1, :], in_=q_scale.unsqueeze(0))
+        nc.sync.dma_start(out=trig[:, 1, :], in_=sin.unsqueeze(1).to_broadcast([T, B, HALF]))
         load_words(4, 8)
         ones = keep.tile([P, P], BF16)
         nc.vector.memset(ones[:], 1.0)
         neg_ones = keep.tile([P, P], BF16)
         nc.vector.memset(neg_ones[:], -1.0)
+        units = keep.tile([P, 2 * HD], BF16)
+        nc.vector.memset(units[:, 0 : HD + HALF], 1.0 / P)
+        nc.vector.memset(units[:, HD + HALF :], -1.0 / P)
         nc.vector.memset(w_scales[1][:].bitcast(I32), 0)
         load_scales(1)
         load_words(8, 12)
@@ -130,29 +134,38 @@ def tile_multiheadattention_pa_s_kernel(tc, q_input, Wq_words, Wq_scales, q_scal
         group_end = {}
         for lo, hi, eng in GROUPS:
             group_end[hi] = (lo, eng)
-        acc_of = {}
+        head_sums = {}
+
+        def one_pass(sums, h, g):
+            nc.tensor.matmul_mx(
+                out=sums,
+                lhsT=x_codes[:, g, :].bitcast(FP8X4),
+                lhsT_scale=x_scales[:, g, :],
+                rhs=w_words[h][:, g, 2 * HD * (h - w_first[h]) : 2 * HD * (h - w_first[h] + 1)].bitcast(FP4X4),
+                rhs_scale=w_scales[h // SCALE_HEADS][:, g, HD * (h % SCALE_HEADS) : HD * (h % SCALE_HEADS + 1)],
+                start=(g == 0),
+                stop=(g == PASSES - 1),
+            )
 
         def passes(pair):
             acc = psum.tile([P, 2, HD], F32, name="acc%d" % pair, tag="bank%d" % BANK_OF_PAIR[pair])
-            acc_of[pair] = acc
             for j in range(2):
-                h = 2 * pair + j
+                head_sums[2 * pair + j] = acc[:, j, :]
                 for g in range(PASSES):
-                    nc.tensor.matmul_mx(
-                        out=acc[:, j, :],
-                        lhsT=x_codes[:, g, :].bitcast(FP8X4),
-                        lhsT_scale=x_scales[:, g, :],
-                        rhs=w_words[h][:, g, 2 * HD * (h - w_first[h]) : 2 * HD * (h - w_first[h] + 1)].bitcast(FP4X4),
-                        rhs_scale=w_scales[h // SCALE_HEADS][
-                            :, g, HD * (h % SCALE_HEADS) : HD * (h % SCALE_HEADS + 1)
-                        ],
-                        start=(g == 0),
-                        stop=(g == PASSES - 1),
-                    )
+                    one_pass(head_sums[2 * pair + j], 2 * pair + j, g)
+
+        def first_passes():
+            acc0 = psum.tile([P, 2, HD], F32, name="acc0", tag="bank%d" % BANK_OF_PAIR[0])
+            acc1 = psum.tile([P, HD], F32, name="acc_head1", tag="bank%d" % BANK_OF_HEAD_1)
+            head_sums[0] = acc0[:, 0, :]
+            head_sums[1] = acc1[:]
+            for g in range(PASSES):
+                for h in range(2):
+                    one_pass(head_sums[h], h, g)
 
         def square(h):
             nc.scalar.activation(
-                out=squares[:, h, :], in_=acc_of[h // 2][:, h % 2, :], func=ACT.Square, accum_out=sumsq[:, h : h + 1]
+                out=squares[:, h, :], in_=head_sums[h], func=ACT.Square, accum_out=sumsq[:, h : h + 1]
             )
 
         def root(pair):
@@ -178,7 +191,7 @@ def tile_multiheadattention_pa_s_kernel(tc, q_input, Wq_words, Wq_scales, q_scal
             for h in (2 * pair, 2 * pair + 1):
                 nc.vector.scalar_tensor_tensor(
                     out=prods[:, h, :, :, :].rearrange("p s f j -> p s (f j)"),
-                    in0=acc_of[pair][:, h % 2, :].unsqueeze(1).to_broadcast([P, 2, HD]),
+                    in0=head_sums[h].unsqueeze(1).to_broadcast([P, 2, HD]),
                     scalar=inv_rms[:, h : h + 1],
                     in1=tables_flat,
                     op0=ALU.mult,
@@ -195,28 +208,21 @@ def tile_multiheadattention_pa_s_kernel(tc, q_input, Wq_words, Wq_scales, q_scal
                     )
                     store(lo, h + 1)
 
-        passes(0)
+        spread = psum.tile([P, 2 * HD], F32, name="spread", tag="bank7")
+        nc.tensor.matmul(out=spread[:], lhsT=ones[:], rhs=units[:], start=True, stop=False)
+        nc.tensor.matmul(out=spread[:, 0:HD], lhsT=ones[:], rhs=q_scale_row[:], start=False, stop=False)
+        nc.tensor.matmul(out=spread[:, HD : HD + HALF], lhsT=ones[:], rhs=q_scale_row[:, 0:HALF], start=False, stop=False)
+        nc.tensor.matmul(out=spread[:, HD + HALF :], lhsT=neg_ones[:], rhs=q_scale_row[:, HALF:HD], start=False, stop=True)
+        first_passes()
 
-        spread = psum.tile([P, HD + HALF], F32, name="spread", tag="bank7")
-        q_scale_ps = spread[:, 0:HD]
-        nc.tensor.matmul(out=q_scale_ps, lhsT=ones[:], rhs=q_scale_row[:], start=True, stop=True)
-        neg_ps = spread[:, HD : HD + HALF]
-        nc.tensor.matmul(out=neg_ps, lhsT=neg_ones[:], rhs=q_scale_row[:, HALF:HD], start=True, stop=True)
         tables = keep.tile([P, 2, 2, HALF], F32)
-        nc.vector.scalar_tensor_tensor(
-            out=tables[:, 0, :, :],
-            in0=q_scale_ps.rearrange("p (f j) -> p f j", f=2),
-            scalar=1.0,
-            in1=trig[:, 0, :].unsqueeze(1).to_broadcast([P, 2, HALF]),
-            op0=ALU.add,
-            op1=ALU.mult,
-        )
-        nc.vector.scalar_tensor_tensor(
-            out=tables[:, 1, 0, :], in0=q_scale_ps[:, 0:HALF], scalar=1.0, in1=trig[:, 1, :], op0=ALU.add, op1=ALU.mult
-        )
-        nc.vector.scalar_tensor_tensor(
-            out=tables[:, 1, 1, :], in0=neg_ps, scalar=-1.0, in1=trig[:, 1, :], op0=ALU.add, op1=ALU.mult
-        )
+        for s in range(2):
+            nc.vector.tensor_tensor(
+                out=tables[:, s, :, :],
+                in0=spread[:, HD * s : HD * (s + 1)].rearrange("p (f j) -> p f j", f=2),
+                in1=trig[:, s, :].unsqueeze(1).to_broadcast([P, 2, HALF]),
+                op=ALU.mult,
+            )
         tables_flat = tables[:].rearrange("p s f j -> p s (f j)")
 
         square(0)

@@ -71,15 +71,17 @@ def tile_multiheadattention_pa_s_kernel(tc, q_input, Wq_words, Wq_scales, q_scal
             )
 
         make_identity(nc, ident[:])
+        nc.gpsimd.dma_start(out=trig[:, 0, :], in_=cos.unsqueeze(1).to_broadcast([T, B, HALF]))
         zeros = keep.tile([P, P], F32)
         nc.vector.memset(zeros[:], 0.0)
         one = keep.tile([P, 1], F32)
         nc.vector.memset(one[:], 1.0)
         nc.vector.memset(q_scale_row[:], 0.0)
         nc.vector.memset(w_scales[0][:].bitcast(I32), 0)
-        nc.scalar.dma_start(out=trig[:, 0, :], in_=cos.unsqueeze(1).to_broadcast([T, B, HALF]))
+        for g, queue in ((0, nc.sync), (1, nc.scalar)):
+            k_cols = slice(K_PASS * g, K_PASS * (g + 1))
+            queue.dma_start(out=x_sb[:, k_cols], in_=q_input[:, :, k_cols].rearrange("b t k -> t b k"))
         nc.scalar.dma_start(out=q_scale_row[0:1, :], in_=q_scale.unsqueeze(0))
-        nc.sync.dma_start(out=x_sb[:], in_=q_input.rearrange("b t k -> t b k"))
         load_words(0, 4)
         load_scales(0)
         nc.sync.dma_start(out=trig[:, 1, :], in_=sin.unsqueeze(1).to_broadcast([T, B, HALF]))

@@ -26,7 +26,8 @@ W_CHUNKS = [[0,4],[4,8],[8,12],[12,16]]
 SCALE_HEADS = 8
 BANK_OF_PAIR = [2,4,5,6,7,0,1,2]
 BANK_OF_HEAD_1 = 3
-GROUPS = [[0,2,'g'],[2,5,'g'],[5,8,'g'],[8,11,'g'],[11,13,'g'],[13,16,'v']]
+GROUPS = [[0,2],[2,4],[6,8],[8,10],[10,13]]
+PE_PAIR = 2
 AHEAD = 1
 
 FLOPS = 2 * B * T * D * N_OUT
@@ -134,8 +135,8 @@ def tile_multiheadattention_pa_s_kernel(tc, q_input, Wq_words, Wq_scales, q_scal
         prods = keep.tile([P, H, 2, 2, HALF], F32)
         o_sb = keep.tile([P, H, 2, HALF], F32)
         group_end = {}
-        for lo, hi, eng in GROUPS:
-            group_end[hi] = (lo, eng)
+        for lo, hi in GROUPS:
+            group_end[hi] = lo
         head_sums = {}
 
         def one_pass(sums, h, g):
@@ -200,15 +201,19 @@ def tile_multiheadattention_pa_s_kernel(tc, q_input, Wq_words, Wq_scales, q_scal
                     op1=ALU.mult,
                 )
                 if h + 1 in group_end:
-                    lo, eng = group_end[h + 1]
-                    adder = nc.gpsimd if eng == "g" else nc.vector
-                    adder.tensor_tensor(
-                        out=o_sb[:, lo : h + 1, :, :],
-                        in0=prods[:, lo : h + 1, 0, :, :],
-                        in1=prods[:, lo : h + 1, 1, ::-1, :],
-                        op=ALU.add,
-                    )
-                    store(lo, h + 1)
+                    add(nc.gpsimd, group_end[h + 1], h + 1)
+
+        def add(adder, lo, hi):
+            adder.tensor_tensor(
+                out=o_sb[:, lo:hi, :, :], in0=prods[:, lo:hi, 0, :, :], in1=prods[:, lo:hi, 1, ::-1, :], op=ALU.add
+            )
+
+        def add_in_psum(pair):
+            heads = slice(2 * pair, 2 * pair + 2)
+            total = psum.tile([P, 2, 2, HALF], F32, name="total", tag="bank%d" % BANK_OF_HEAD_1)
+            nc.tensor.matmul(out=total[:], lhsT=ident[:], rhs=prods[:, heads, 0, :, :], start=True, stop=False)
+            nc.tensor.matmul(out=total[:], lhsT=ident[:], rhs=prods[:, heads, 1, ::-1, :], start=False, stop=True)
+            nc.scalar.copy(out=o_sb[:, heads, :, :], in_=total[:])
 
         spread = psum.tile([P, 2 * HD], F32, name="spread", tag="bank7")
         nc.tensor.matmul(out=spread[:], lhsT=ones[:], rhs=units[:], start=True, stop=False)
@@ -231,6 +236,7 @@ def tile_multiheadattention_pa_s_kernel(tc, q_input, Wq_words, Wq_scales, q_scal
         square(1)
         root(0)
         products(0)
+        store(0, 2)
         squared = 2
         issued = 1
         for pair in range(1, PAIRS):
@@ -242,4 +248,13 @@ def tile_multiheadattention_pa_s_kernel(tc, q_input, Wq_words, Wq_scales, q_scal
                 square(squared)
                 squared += 1
             root(pair)
+            if pair == PAIRS - 1:
+                add_in_psum(PE_PAIR)
+                store(4, 8)
+                store(8, 10)
+                store(10, 13)
             products(pair)
+            if pair == 1:
+                store(2, 4)
+        add(nc.vector, 13, 16)
+        store(13, 16)

from contextlib import ExitStack

import concourse.mybir as mybir
from concourse.masks import make_identity

F32 = mybir.dt.float32
BF16 = mybir.dt.bfloat16
I32 = mybir.dt.int32
U32 = mybir.dt.uint32
U8 = mybir.dt.uint8
FP8X4 = mybir.dt.float8_e4m3fn_x4
FP4X4 = mybir.dt.float4_e2m1fn_x4
ALU = mybir.AluOpType
ACT = mybir.ActivationFunctionType

B, T, D, H, HD = 2, 64, 1024, 16, 128
HALF = HD // 2
EPS = 1e-6
P = 128
K_PASS = 512
PASSES = D // K_PASS
N_OUT = H * HD
PAIRS = H // 2

W_CHUNKS = [[0,4],[4,8],[8,12],[12,16]]
SCALE_HEADS = 8
BANK_OF_PAIR = [2,4,5,6,7,0,1,2]
BANK_OF_HEAD_1 = 3
GROUPS = [[0,2],[2,4],[6,8],[8,10],[10,13]]
PE_PAIR = 2
AHEAD = 1

FLOPS = 2 * B * T * D * N_OUT


def tile_multiheadattention_pa_s_kernel(tc, q_input, Wq_words, Wq_scales, q_scale, cos, sin, out):
    nc = tc.nc
    with ExitStack() as ctx:
        keep = ctx.enter_context(tc.tile_pool(name="keep", bufs=1))
        psum = ctx.enter_context(tc.psum_pool(name="psum", bufs=1))
        ctx.enter_context(tc.manual_schedule())

        q_scale_row = keep.tile([P, HD], BF16)
        x_sb = keep.tile([P, D], BF16)
        w_scales = [
            keep.tile([P, PASSES, HD * SCALE_HEADS], U8, name="w_scales%d" % s, align_bytes=64)
            for s in range(H // SCALE_HEADS)
        ]
        w_words = {}
        w_first = {}
        for lo, hi in W_CHUNKS:
            chunk = keep.tile([P, PASSES, 2 * HD * (hi - lo)], U8, name="w_words%d" % lo, align_bytes=64)
            for h in range(lo, hi):
                w_words[h] = chunk
                w_first[h] = lo
        trig = keep.tile([P, 2, HALF], BF16)
        ident = keep.tile([P, P], F32)

        def load_scales(s):
            n_cols = slice(HD * SCALE_HEADS * s, HD * SCALE_HEADS * (s + 1))
            for r in range(4):
                nc.sync.dma_start(
                    out=w_scales[s][:].bitcast(I32)[r:P:32],
                    in_=Wq_scales[:, r:16:4, n_cols].bitcast(I32).rearrange("g q n -> q g n"),
                )

        def load_words(lo, hi):
            w_bytes = slice(2 * HD * lo, 2 * HD * hi)
            nc.sync.dma_start(
                out=w_words[lo][:].bitcast(I32),
                in_=Wq_words[:, :, w_bytes].bitcast(I32).rearrange("g p n -> p g n"),
            )

        make_identity(nc, ident[:])
        nc.gpsimd.dma_start(out=trig[:, 0, :], in_=cos.unsqueeze(1).to_broadcast([T, B, HALF]))
        zeros = keep.tile([P, P], F32)
        nc.vector.memset(zeros[:], 0.0)
        one = keep.tile([P, 1], F32)
        nc.vector.memset(one[:], 1.0)
        nc.vector.memset(q_scale_row[:], 0.0)
        nc.vector.memset(w_scales[0][:].bitcast(I32), 0)
        for g, queue in ((0, nc.sync), (1, nc.scalar)):
            k_cols = slice(K_PASS * g, K_PASS * (g + 1))
            queue.dma_start(out=x_sb[:, k_cols], in_=q_input[:, :, k_cols].rearrange("b t k -> t b k"))
        nc.scalar.dma_start(out=q_scale_row[0:1, :], in_=q_scale.unsqueeze(0))
        load_words(0, 4)
        load_scales(0)
        nc.sync.dma_start(out=trig[:, 1, :], in_=sin.unsqueeze(1).to_broadcast([T, B, HALF]))
        load_words(4, 8)
        ones = keep.tile([P, P], BF16)
        nc.vector.memset(ones[:], 1.0)
        neg_ones = keep.tile([P, P], BF16)
        nc.vector.memset(neg_ones[:], -1.0)
        units = keep.tile([P, 2 * HD], BF16)
        nc.vector.memset(units[:, 0 : HD + HALF], 1.0 / P)
        nc.vector.memset(units[:, HD + HALF :], -1.0 / P)
        nc.vector.memset(w_scales[1][:].bitcast(I32), 0)
        load_scales(1)
        load_words(8, 12)
        load_words(12, 16)

        unused = keep.tile([P, 1], F32)
        nc.scalar.activation(out=unused[:], in_=one[:], func=ACT.Abs_reciprocal_sqrt)

        warm = psum.tile([P, P], F32, name="warm", tag="bank6")

        def dummy_matmuls(count):
            for n in range(count):
                nc.tensor.matmul(out=warm[:], lhsT=zeros[:], rhs=zeros[:], start=True, stop=True)

        dummy_matmuls(2)

        x_words = x_sb[:].bitcast(F32)
        grouped = keep.tile([P, PASSES, 4 * P], BF16, align_bytes=64)
        x_codes = keep.tile([P, PASSES, P], U32, align_bytes=64)
        x_scales = keep.tile([P, PASSES, P], U8, align_bytes=64)
        copy_out = [nc.vector.tensor_copy, nc.scalar.copy]
        front = [
            psum.tile([P, 2, P], F32, name="front0", tag="bank0"),
            psum.tile([P, 2, P], F32, name="front1", tag="bank1"),
        ]
        for g in range(PASSES):
            xT = front[g]
            for u in range(2):
                nc.tensor.transpose(xT[:, u, :], x_words[:, 256 * g + u : 256 * (g + 1) : 2], ident[:])
            copy_out[g](
                out=grouped[:, g, :].bitcast(F32).rearrange("p (m u) -> p m u", u=2),
                in_=xT[:].rearrange("p u m -> p m u"),
            )
            nc.vector.quantize_mx(out=x_codes[:, g, :].bitcast(FP8X4), scales=x_scales[:, g, :], in_=grouped[:, g, :])

        squares = keep.tile([P, H, HD], F32)
        sumsq = keep.tile([P, H], F32)
        inv_rms = keep.tile([P, H], F32)
        prods = keep.tile([P, H, 2, 2, HALF], F32)
        o_sb = keep.tile([P, H, 2, HALF], F32)
        group_end = {}
        for lo, hi in GROUPS:
            group_end[hi] = lo
        head_sums = {}

        def one_pass(sums, h, g):
            nc.tensor.matmul_mx(
                out=sums,
                lhsT=x_codes[:, g, :].bitcast(FP8X4),
                lhsT_scale=x_scales[:, g, :],
                rhs=w_words[h][:, g, 2 * HD * (h - w_first[h]) : 2 * HD * (h - w_first[h] + 1)].bitcast(FP4X4),
                rhs_scale=w_scales[h // SCALE_HEADS][:, g, HD * (h % SCALE_HEADS) : HD * (h % SCALE_HEADS + 1)],
                start=(g == 0),
                stop=(g == PASSES - 1),
            )

        def passes(pair):
            acc = psum.tile([P, 2, HD], F32, name="acc%d" % pair, tag="bank%d" % BANK_OF_PAIR[pair])
            for j in range(2):
                head_sums[2 * pair + j] = acc[:, j, :]
                for g in range(PASSES):
                    one_pass(head_sums[2 * pair + j], 2 * pair + j, g)

        def first_passes():
            acc0 = psum.tile([P, 2, HD], F32, name="acc0", tag="bank%d" % BANK_OF_PAIR[0])
            acc1 = psum.tile([P, HD], F32, name="acc_head1", tag="bank%d" % BANK_OF_HEAD_1)
            head_sums[0] = acc0[:, 0, :]
            head_sums[1] = acc1[:]
            for g in range(PASSES):
                for h in range(2):
                    one_pass(head_sums[h], h, g)

        def square(h):
            nc.scalar.activation(
                out=squares[:, h, :], in_=head_sums[h], func=ACT.Square, accum_out=sumsq[:, h : h + 1]
            )

        def root(pair):
            these = slice(2 * pair, 2 * pair + 2)
            nc.scalar.activation(
                out=inv_rms[:, these], in_=sumsq[:, these], func=ACT.Abs_reciprocal_sqrt, scale=1.0 / HD, bias=EPS
            )

        def store(lo, hi):
            heads = slice(lo, hi)
            if hi - lo == 1:
                nc.sync.dma_start(
                    out=out[:, lo, :, :].rearrange("b t d -> t b d"), in_=o_sb[:, lo, :, :].rearrange("p f j -> p (f j)")
                )
            else:
                for b in range(B):
                    nc.sync.dma_start(
                        out=out[b, heads, :, :].rearrange("h t d -> t h d"),
                        in_=o_sb[b:P:B, heads, :, :].rearrange("p h f j -> p h (f j)"),
                    )

        def products(pair):
            for h in (2 * pair, 2 * pair + 1):
                nc.vector.scalar_tensor_tensor(
                    out=prods[:, h, :, :, :].rearrange("p s f j -> p s (f j)"),
                    in0=head_sums[h].unsqueeze(1).to_broadcast([P, 2, HD]),
                    scalar=inv_rms[:, h : h + 1],
                    in1=tables_flat,
                    op0=ALU.mult,
                    op1=ALU.mult,
                )
                if h + 1 in group_end:
                    add(nc.gpsimd, group_end[h + 1], h + 1)

        def add(adder, lo, hi):
            adder.tensor_tensor(
                out=o_sb[:, lo:hi, :, :], in0=prods[:, lo:hi, 0, :, :], in1=prods[:, lo:hi, 1, ::-1, :], op=ALU.add
            )

        def add_in_psum(pair):
            heads = slice(2 * pair, 2 * pair + 2)
            total = psum.tile([P, 2, 2, HALF], F32, name="total", tag="bank%d" % BANK_OF_HEAD_1)
            nc.tensor.matmul(out=total[:], lhsT=ident[:], rhs=prods[:, heads, 0, :, :], start=True, stop=False)
            nc.tensor.matmul(out=total[:], lhsT=ident[:], rhs=prods[:, heads, 1, ::-1, :], start=False, stop=True)
            nc.scalar.copy(out=o_sb[:, heads, :, :], in_=total[:])

        spread = psum.tile([P, 2 * HD], F32, name="spread", tag="bank7")
        nc.tensor.matmul(out=spread[:], lhsT=ones[:], rhs=units[:], start=True, stop=False)
        nc.tensor.matmul(out=spread[:, 0:HD], lhsT=ones[:], rhs=q_scale_row[:], start=False, stop=False)
        nc.tensor.matmul(out=spread[:, HD : HD + HALF], lhsT=ones[:], rhs=q_scale_row[:, 0:HALF], start=False, stop=False)
        nc.tensor.matmul(out=spread[:, HD + HALF :], lhsT=neg_ones[:], rhs=q_scale_row[:, HALF:HD], start=False, stop=True)
        first_passes()

        tables = keep.tile([P, 2, 2, HALF], F32)
        for s in range(2):
            nc.vector.tensor_tensor(
                out=tables[:, s, :, :],
                in0=spread[:, HD * s : HD * (s + 1)].rearrange("p (f j) -> p f j", f=2),
                in1=trig[:, s, :].unsqueeze(1).to_broadcast([P, 2, HALF]),
                op=ALU.mult,
            )
        tables_flat = tables[:].rearrange("p s f j -> p s (f j)")

        square(0)
        square(1)
        root(0)
        products(0)
        store(0, 2)
        squared = 2
        issued = 1
        for pair in range(1, PAIRS):
            upto = min(H, 2 * pair + 2 + (AHEAD if pair > 1 else 0))
            while squared < upto:
                if squared // 2 >= issued:
                    passes(issued)
                    issued += 1
                square(squared)
                squared += 1
            root(pair)
            if pair == PAIRS - 1:
                add_in_psum(PE_PAIR)
                store(4, 8)
                store(8, 10)
                store(10, 13)
            products(pair)
            if pair == 1:
                store(2, 4)
        add(nc.vector, 13, 16)
        store(13, 16)
